import numpy as np
import ml_dtypes


def mxq(x, axis, fmt="e4m3"):
    dtype, down = {"e4m3": (ml_dtypes.float8_e4m3fn, 7), "e5m2": (ml_dtypes.float8_e5m2, 14)}[fmt]
    v = np.moveaxis(np.asarray(x, np.float32).astype(ml_dtypes.bfloat16).astype(np.float64), axis, -1)
    blocks = v.reshape(v.shape[:-1] + (-1, 32))
    amax = np.abs(blocks).max(-1, keepdims=True)
    byte = np.maximum(np.where(amax > 0, np.frexp(amax)[1] - 1 + 127, 0) - down, 1)
    scale = np.exp2(byte - 127.0)
    codes = (blocks / scale).astype(np.float32).astype(dtype).astype(np.float64)
    return np.moveaxis((codes * scale).reshape(v.shape), -1, axis)


WIDE = False


def mx_kscale(k):
    if not WIDE:
        return np.ones(k)
    levels = np.array([10, -10, 5, -5, 0])
    a = np.random.permutation(np.resize(levels, k // 512 * 4)).reshape(k // 512, 4)
    idx = np.arange(k)
    return np.exp2(a[idx // 512, idx % 128 // 32])


BF16 = ml_dtypes.bfloat16


def bf(x):
    return np.asarray(x, np.float32).astype(BF16)


def f64(x):
    return np.asarray(x).astype(np.float64)


B, S, HID, NH, NOPE, ROPE, VD, KV_RANK, SW, QB = 1, 128, 512, 8, 64, 128, 128, 512, 384, 128
QK = NOPE + ROPE


def rotate_half(x):
    h = x.shape[-1] // 2
    return np.concatenate([-x[..., h:], x[..., :h]], axis=-1)


def rope_tables():
    pos = np.arange(S, dtype=np.float64)
    inv = 1.0 / (10000.0 ** (np.arange(0, ROPE, 2, dtype=np.float64) / ROPE))
    ang = pos[:, None] * inv[None, :]
    ang = np.concatenate([ang, ang], axis=-1)
    return bf(np.broadcast_to(np.cos(ang)[None], (B, S, ROPE))), bf(np.broadcast_to(np.sin(ang)[None], (B, S, ROPE)))


def setup_inputs():
    s = mx_kscale(HID)
    cos, sin = rope_tables()
    return {"hidden_states": bf(np.random.standard_normal((B, S, HID)) * s), "cos": cos, "sin": sin,
            "Wq": bf(np.random.standard_normal((HID, NH * QK)) * 2.0 / np.sqrt(HID) / s[:, None]),
            "bq": bf(np.random.standard_normal(NH * QK) * 0.2)}


def reference(hidden_states, cos, sin, Wq, bq):
    q = ((mxq(f64(hidden_states), 2, "e4m3") @ mxq(f64(Wq), 0, "e4m3")) + f64(bq)).reshape(B, S, NH, QK).transpose(0, 2, 1, 3)
    q_nope, q_rope = q[..., :NOPE], q[..., NOPE:]
    c, si = f64(cos)[:, None], f64(sin)[:, None]
    q_rope = q_rope * c + rotate_half(q_rope) * si
    return np.concatenate([q_nope, q_rope], axis=-1)

@@ -1,0 +1,138 @@
+from contextlib import ExitStack
+
+import concourse.mybir as mybir
+from concourse.masks import make_identity
+
+BF16 = mybir.dt.bfloat16
+F32 = mybir.dt.float32
+U32 = mybir.dt.uint32
+U8 = mybir.dt.uint8
+FP8X4 = mybir.dt.float8_e4m3fn_x4
+ALU = mybir.AluOpType
+
+P = 128
+PACK = 4
+HID = P * PACK
+HEADS = 8
+NOPE = 64
+HALF = 64
+ROPE = 2 * HALF
+HEAD = NOPE + ROPE
+GROUP_HEADS = 2
+GROUPS = HEADS // GROUP_HEADS
+GROUP_COLS = GROUP_HEADS * HEAD
+WIDE = 256
+PIECES = ((0, WIDE), (WIDE, GROUP_COLS))
+
+FLOPS = 2 * P * HID * HEADS * HEAD
+
+
+def regroup(engine_copy, grouped, raw, first, last):
+    engine_copy(
+        out=grouped[:, PACK * first : PACK * last].rearrange("p (c i j) -> p c j i", i=4, j=PACK),
+        in_=raw[:, :, first:last].rearrange("p j (c i) -> p c j i", i=4),
+    )
+
+
+def tile_gptossmlaattention_pb_s_kernel(tc, hidden_states, cos, sin, Wq, bq, out):
+    nc = tc.nc
+    with ExitStack() as ctx:
+        keep = ctx.enter_context(tc.tile_pool(name="keep", bufs=1))
+        per_group = ctx.enter_context(tc.tile_pool(name="per_group", bufs=GROUPS))
+        psum_hs = ctx.enter_context(tc.psum_pool(name="psum_hs", bufs=1))
+        psum_q = ctx.enter_context(tc.psum_pool(name="psum_q", bufs=GROUPS))
+
+        hs = keep.tile([P, HID], BF16)
+        nc.sync.dma_start(out=hs[:], in_=hidden_states.rearrange("b s k -> (b s) k"))
+        w_rows = Wq.rearrange("(p j) n -> p j n", j=PACK)
+        w_raw = []
+        for g in range(GROUPS):
+            raw = per_group.tile([P, PACK, GROUP_COLS], BF16, name="raw")
+            nc.sync.dma_start(out=raw[:], in_=w_rows[:, :, g * GROUP_COLS : (g + 1) * GROUP_COLS])
+            w_raw.append(raw)
+        bias = keep.tile([P, HEADS * HEAD], BF16)
+        nc.scalar.dma_start(out=bias[:], in_=bq.partition_broadcast(P))
+        cos_sb = keep.tile([P, ROPE], BF16)
+        nc.scalar.dma_start(out=cos_sb[:], in_=cos.rearrange("b s d -> (b s) d"))
+        sin_rows = sin.rearrange("b s d -> (b s) d")
+        sin_swapped = keep.tile([P, ROPE], BF16)
+        nc.scalar.dma_start(out=sin_swapped[:, 0:HALF], in_=sin_rows[:, HALF:ROPE])
+        nc.scalar.dma_start(out=sin_swapped[:, HALF:ROPE], in_=sin_rows[:, 0:HALF])
+
+        identity = keep.tile([P, P], F32)
+        make_identity(nc, identity[:])
+        hs_words = hs[:].bitcast(F32).rearrange("s (p u) -> s u p", u=2)
+        hs_t = psum_hs.tile([P, 2, P], F32)
+        for u in range(2):
+            nc.tensor.transpose(hs_t[:, u, :], hs_words[:, u, :], identity[:])
+        hs_grouped = keep.tile([P, P * PACK], BF16, align_bytes=64)
+        nc.scalar.copy(
+            out=hs_grouped[:].bitcast(F32).rearrange("p (s u) -> p s u", u=2),
+            in_=hs_t[:].rearrange("p u s -> p s u"),
+        )
+        hs_codes = keep.tile([P, P], U32, align_bytes=64)
+        hs_scales = keep.tile([P, P], U8, align_bytes=64)
+        nc.vector.quantize_mx(out=hs_codes[:].bitcast(FP8X4), scales=hs_scales[:], in_=hs_grouped[:])
+
+        cos_heads = cos_sb[:].unsqueeze(1).to_broadcast([P, GROUP_HEADS, ROPE])
+        sin_heads = sin_swapped[:].unsqueeze(1).to_broadcast([P, GROUP_HEADS, ROPE])
+        out_rows = out.rearrange("b h s d -> s (b h) d")
+
+        def project(g):
+            grouped = per_group.tile([P, GROUP_COLS * PACK], BF16, align_bytes=64, name="grouped")
+            codes = per_group.tile([P, GROUP_COLS], U32, align_bytes=64, name="codes")
+            scales = per_group.tile([P, GROUP_COLS], U8, align_bytes=64, name="scales")
+            acc = psum_q.tile([P, GROUP_COLS], F32, name="acc")
+            for first, last in PIECES:
+                if g == 0 and first == 0:
+                    regroup(nc.vector.tensor_copy, grouped, w_raw[g], first, last)
+                else:
+                    regroup(nc.scalar.copy, grouped, w_raw[g], first, last)
+            for first, last in PIECES:
+                nc.vector.quantize_mx(
+                    out=codes[:, first:last].bitcast(FP8X4),
+                    scales=scales[:, first:last],
+                    in_=grouped[:, PACK * first : PACK * last],
+                )
+                nc.tensor.matmul_mx(
+                    out=acc[:, first:last],
+                    lhsT=hs_codes[:].bitcast(FP8X4),
+                    lhsT_scale=hs_scales[:],
+                    rhs=codes[:, first:last].bitcast(FP8X4),
+                    rhs_scale=scales[:, first:last],
+                    start=True,
+                    stop=True,
+                )
+            return acc
+
+        def finish(g, acc):
+            q = per_group.tile([P, GROUP_HEADS, HEAD], F32, name="q")
+            nc.vector.tensor_tensor(
+                out=q[:].rearrange("p h d -> p (h d)"),
+                in0=acc[:],
+                in1=bias[:, g * GROUP_COLS : (g + 1) * GROUP_COLS],
+                op=ALU.add,
+            )
+            by_cos = per_group.tile([P, GROUP_HEADS, ROPE], F32, name="by_cos")
+            by_sin = per_group.tile([P, GROUP_HEADS, ROPE], F32, name="by_sin")
+            nc.vector.tensor_tensor(out=by_cos[:], in0=q[:, :, NOPE:HEAD], in1=cos_heads, op=ALU.mult)
+            nc.vector.tensor_tensor(out=by_sin[:], in0=q[:, :, NOPE:HEAD], in1=sin_heads, op=ALU.mult)
+            nc.vector.tensor_tensor(
+                out=q[:, :, NOPE : NOPE + HALF],
+                in0=by_cos[:, :, 0:HALF],
+                in1=by_sin[:, :, HALF:ROPE],
+                op=ALU.subtract,
+            )
+            nc.vector.tensor_tensor(
+                out=q[:, :, NOPE + HALF : HEAD],
+                in0=by_cos[:, :, HALF:ROPE],
+                in1=by_sin[:, :, 0:HALF],
+                op=ALU.add,
+            )
+            nc.sync.dma_start(out=out_rows[:, g * GROUP_HEADS : (g + 1) * GROUP_HEADS, :], in_=q[:])
+
+        accs = [project(0)]
+        for g in range(GROUPS):
+            if g + 1 < GROUPS:
+                accs.append(project(g + 1))
+            finish(g, accs[g])

@@ -23,6 +23,8 @@ GROUPS = HEADS // GROUP_HEADS
 GROUP_COLS = GROUP_HEADS * HEAD
 WIDE = 256
 PIECES = ((0, WIDE), (WIDE, GROUP_COLS))
+BIAS_ROWS = HEADS * HEAD // (2 * P)
+BANK_ROWS = 4
 
 FLOPS = 2 * P * HID * HEADS * HEAD
 
@@ -40,6 +42,7 @@ def tile_gptossmlaattention_pb_s_kernel(tc, hidden_states, cos, sin, Wq, bq, out
         keep = ctx.enter_context(tc.tile_pool(name="keep", bufs=1))
         per_group = ctx.enter_context(tc.tile_pool(name="per_group", bufs=GROUPS))
         psum_hs = ctx.enter_context(tc.psum_pool(name="psum_hs", bufs=1))
+        psum_bias = ctx.enter_context(tc.psum_pool(name="psum_bias", bufs=2))
         psum_q = ctx.enter_context(tc.psum_pool(name="psum_q", bufs=GROUPS))
 
         hs = keep.tile([P, HID], BF16)
@@ -50,8 +53,9 @@ def tile_gptossmlaattention_pb_s_kernel(tc, hidden_states, cos, sin, Wq, bq, out
             raw = per_group.tile([P, PACK, GROUP_COLS], BF16, name="raw")
             nc.sync.dma_start(out=raw[:], in_=w_rows[:, :, g * GROUP_COLS : (g + 1) * GROUP_COLS])
             w_raw.append(raw)
-        bias = keep.tile([P, HEADS * HEAD], BF16)
-        nc.scalar.dma_start(out=bias[:], in_=bq.partition_broadcast(P))
+        bias_rows = keep.tile([P, 2 * P], BF16)
+        nc.vector.memset(bias_rows[:], 0.0)
+        nc.scalar.dma_start(out=bias_rows[0:BIAS_ROWS, :], in_=bq.rearrange("(r c) -> r c", c=2 * P))
         cos_sb = keep.tile([P, ROPE], BF16)
         nc.scalar.dma_start(out=cos_sb[:], in_=cos.rearrange("b s d -> (b s) d"))
         sin_rows = sin.rearrange("b s d -> (b s) d")
@@ -73,6 +77,23 @@ def tile_gptossmlaattention_pb_s_kernel(tc, hidden_states, cos, sin, Wq, bq, out
         hs_codes = keep.tile([P, P], U32, align_bytes=64)
         hs_scales = keep.tile([P, P], U8, align_bytes=64)
         nc.vector.quantize_mx(out=hs_codes[:].bitcast(FP8X4), scales=hs_scales[:], in_=hs_grouped[:])
+
+        bias_turned = psum_hs.tile([P, P], F32)
+        nc.tensor.transpose(bias_turned[:], bias_rows[:].bitcast(F32), identity[:])
+        bias_cols = keep.tile([P, BIAS_ROWS], F32)
+        nc.vector.tensor_copy(out=bias_cols[:], in_=bias_turned[:, 0:BIAS_ROWS])
+        bias = keep.tile([P, HEADS * HEAD], BF16)
+        bias_words = bias[:].bitcast(F32)
+        for first_row in range(0, BIAS_ROWS, BANK_ROWS):
+            rows = min(BANK_ROWS, BIAS_ROWS - first_row)
+            spread = psum_bias.tile([P, BANK_ROWS, P], F32, name="spread")
+            for r in range(rows):
+                column = bias_cols[:, first_row + r : first_row + r + 1]
+                nc.tensor.transpose(spread[:, r, :], column.to_broadcast([P, P]), identity[:])
+            nc.scalar.copy(
+                out=bias_words[:, first_row * P : (first_row + rows) * P],
+                in_=spread[:, 0:rows, :].rearrange("p r c -> p (r c)"),
+            )
 
         cos_heads = cos_sb[:].unsqueeze(1).to_broadcast([P, GROUP_HEADS, ROPE])
         sin_heads = sin_swapped[:].unsqueeze(1).to_broadcast([P, GROUP_HEADS, ROPE])

@@ -23,25 +23,20 @@ GROUPS = HEADS // GROUP_HEADS
 GROUP_COLS = GROUP_HEADS * HEAD
 WIDE = 256
 PIECES = ((0, WIDE), (WIDE, GROUP_COLS))
+VECTOR_GROUPS = 2
 BIAS_ROWS = HEADS * HEAD // (2 * P)
 BANK_ROWS = 4
 
 FLOPS = 2 * P * HID * HEADS * HEAD
 
 
-def regroup(engine_copy, grouped, raw, first, last):
-    engine_copy(
-        out=grouped[:, PACK * first : PACK * last].rearrange("p (c i j) -> p c j i", i=4, j=PACK),
-        in_=raw[:, :, first:last].rearrange("p j (c i) -> p c j i", i=4),
-    )
-
-
 def tile_gptossmlaattention_pb_s_kernel(tc, hidden_states, cos, sin, Wq, bq, out):
     nc = tc.nc
     with ExitStack() as ctx:
+        ctx.enter_context(tc.manual_schedule())
         keep = ctx.enter_context(tc.tile_pool(name="keep", bufs=1))
         per_group = ctx.enter_context(tc.tile_pool(name="per_group", bufs=GROUPS))
-        psum_hs = ctx.enter_context(tc.psum_pool(name="psum_hs", bufs=1))
+        psum_turn = ctx.enter_context(tc.psum_pool(name="psum_turn", bufs=1))
         psum_bias = ctx.enter_context(tc.psum_pool(name="psum_bias", bufs=2))
         psum_q = ctx.enter_context(tc.psum_pool(name="psum_q", bufs=GROUPS))
 
@@ -66,54 +61,66 @@ def tile_gptossmlaattention_pb_s_kernel(tc, hidden_states, cos, sin, Wq, bq, out
         identity = keep.tile([P, P], F32)
         make_identity(nc, identity[:])
         hs_words = hs[:].bitcast(F32).rearrange("s (p u) -> s u p", u=2)
-        hs_t = psum_hs.tile([P, 2, P], F32)
+        hs_turned = psum_turn.tile([P, 2, P], F32)
         for u in range(2):
-            nc.tensor.transpose(hs_t[:, u, :], hs_words[:, u, :], identity[:])
+            nc.tensor.transpose(hs_turned[:, u, :], hs_words[:, u, :], identity[:])
         hs_grouped = keep.tile([P, P * PACK], BF16, align_bytes=64)
         nc.scalar.copy(
             out=hs_grouped[:].bitcast(F32).rearrange("p (s u) -> p s u", u=2),
-            in_=hs_t[:].rearrange("p u s -> p s u"),
+            in_=hs_turned[:].rearrange("p u s -> p s u"),
         )
-        hs_codes = keep.tile([P, P], U32, align_bytes=64)
-        hs_scales = keep.tile([P, P], U8, align_bytes=64)
-        nc.vector.quantize_mx(out=hs_codes[:].bitcast(FP8X4), scales=hs_scales[:], in_=hs_grouped[:])
 
-        bias_turned = psum_hs.tile([P, P], F32)
+        bias_turned = psum_turn.tile([P, P], F32)
         nc.tensor.transpose(bias_turned[:], bias_rows[:].bitcast(F32), identity[:])
         bias_cols = keep.tile([P, BIAS_ROWS], F32)
         nc.vector.tensor_copy(out=bias_cols[:], in_=bias_turned[:, 0:BIAS_ROWS])
-        bias = keep.tile([P, HEADS * HEAD], BF16)
-        bias_words = bias[:].bitcast(F32)
+        bias_banks = []
         for first_row in range(0, BIAS_ROWS, BANK_ROWS):
             rows = min(BANK_ROWS, BIAS_ROWS - first_row)
             spread = psum_bias.tile([P, BANK_ROWS, P], F32, name="spread")
             for r in range(rows):
                 column = bias_cols[:, first_row + r : first_row + r + 1]
                 nc.tensor.transpose(spread[:, r, :], column.to_broadcast([P, P]), identity[:])
-            nc.scalar.copy(
-                out=bias_words[:, first_row * P : (first_row + rows) * P],
-                in_=spread[:, 0:rows, :].rearrange("p r c -> p (r c)"),
-            )
+            bias_banks.append((first_row, rows, spread))
+        bias = keep.tile([P, HEADS * HEAD], BF16)
 
+        def copy_bias_out():
+            for first_row, rows, spread in bias_banks:
+                nc.scalar.copy(
+                    out=bias[:].bitcast(F32)[:, first_row * P : (first_row + rows) * P],
+                    in_=spread[:, 0:rows, :].rearrange("p r c -> p (r c)"),
+                )
+
+        w_grouped = []
+        accs = []
+        qs = []
+        products = []
         cos_heads = cos_sb[:].unsqueeze(1).to_broadcast([P, GROUP_HEADS, ROPE])
         sin_heads = sin_swapped[:].unsqueeze(1).to_broadcast([P, GROUP_HEADS, ROPE])
         out_rows = out.rearrange("b h s d -> s (b h) d")
 
-        def project(g):
+        def regroup(g):
             grouped = per_group.tile([P, GROUP_COLS * PACK], BF16, align_bytes=64, name="grouped")
+            for first, last in PIECES:
+                by_vector = g < VECTOR_GROUPS and first == 0
+                copy = nc.vector.tensor_copy if by_vector else nc.scalar.copy
+                copy(
+                    out=grouped[:, PACK * first : PACK * last].rearrange(
+                        "p (c i j) -> p c j i", i=4, j=PACK
+                    ),
+                    in_=w_raw[g][:, :, first:last].rearrange("p j (c i) -> p c j i", i=4),
+                )
+            w_grouped.append(grouped)
+
+        def project(g):
             codes = per_group.tile([P, GROUP_COLS], U32, align_bytes=64, name="codes")
             scales = per_group.tile([P, GROUP_COLS], U8, align_bytes=64, name="scales")
             acc = psum_q.tile([P, GROUP_COLS], F32, name="acc")
             for first, last in PIECES:
-                if g == 0 and first == 0:
-                    regroup(nc.vector.tensor_copy, grouped, w_raw[g], first, last)
-                else:
-                    regroup(nc.scalar.copy, grouped, w_raw[g], first, last)
-            for first, last in PIECES:
                 nc.vector.quantize_mx(
                     out=codes[:, first:last].bitcast(FP8X4),
                     scales=scales[:, first:last],
-                    in_=grouped[:, PACK * first : PACK * last],
+                    in_=w_grouped[g][:, PACK * first : PACK * last],
                 )
                 nc.tensor.matmul_mx(
                     out=acc[:, first:last],
@@ -124,36 +131,57 @@ def tile_gptossmlaattention_pb_s_kernel(tc, hidden_states, cos, sin, Wq, bq, out
                     start=True,
                     stop=True,
                 )
-            return acc
+            accs.append(acc)
 
-        def finish(g, acc):
+        def add_bias(g):
             q = per_group.tile([P, GROUP_HEADS, HEAD], F32, name="q")
             nc.vector.tensor_tensor(
                 out=q[:].rearrange("p h d -> p (h d)"),
-                in0=acc[:],
+                in0=accs[g][:],
                 in1=bias[:, g * GROUP_COLS : (g + 1) * GROUP_COLS],
                 op=ALU.add,
             )
+            qs.append(q)
+
+        def multiply_by_tables(g):
             by_cos = per_group.tile([P, GROUP_HEADS, ROPE], F32, name="by_cos")
             by_sin = per_group.tile([P, GROUP_HEADS, ROPE], F32, name="by_sin")
-            nc.vector.tensor_tensor(out=by_cos[:], in0=q[:, :, NOPE:HEAD], in1=cos_heads, op=ALU.mult)
-            nc.vector.tensor_tensor(out=by_sin[:], in0=q[:, :, NOPE:HEAD], in1=sin_heads, op=ALU.mult)
+            x = qs[g][:, :, NOPE:HEAD]
+            nc.vector.tensor_tensor(out=by_cos[:], in0=x, in1=cos_heads, op=ALU.mult)
+            nc.vector.tensor_tensor(out=by_sin[:], in0=x, in1=sin_heads, op=ALU.mult)
+            products.append((by_cos, by_sin))
+
+        def combine_and_store(g):
+            by_cos, by_sin = products[g]
             nc.vector.tensor_tensor(
-                out=q[:, :, NOPE : NOPE + HALF],
+                out=qs[g][:, :, NOPE : NOPE + HALF],
                 in0=by_cos[:, :, 0:HALF],
                 in1=by_sin[:, :, HALF:ROPE],
                 op=ALU.subtract,
             )
             nc.vector.tensor_tensor(
-                out=q[:, :, NOPE + HALF : HEAD],
+                out=qs[g][:, :, NOPE + HALF : HEAD],
                 in0=by_cos[:, :, HALF:ROPE],
                 in1=by_sin[:, :, 0:HALF],
                 op=ALU.add,
             )
-            nc.sync.dma_start(out=out_rows[:, g * GROUP_HEADS : (g + 1) * GROUP_HEADS, :], in_=q[:])
+            nc.sync.dma_start(
+                out=out_rows[:, g * GROUP_HEADS : (g + 1) * GROUP_HEADS, :], in_=qs[g][:]
+            )
 
-        accs = [project(0)]
+        regroup(0)
+        copy_bias_out()
+        hs_codes = keep.tile([P, P], U32, align_bytes=64)
+        hs_scales = keep.tile([P, P], U8, align_bytes=64)
+        nc.vector.quantize_mx(out=hs_codes[:].bitcast(FP8X4), scales=hs_scales[:], in_=hs_grouped[:])
+        project(0)
+        for g in range(1, GROUPS):
+            regroup(g)
         for g in range(GROUPS):
+            add_bias(g)
+            if g > 0:
+                combine_and_store(g - 1)
             if g + 1 < GROUPS:
-                accs.append(project(g + 1))
-            finish(g, accs[g])
+                project(g + 1)
+            multiply_by_tables(g)
+        combine_and_store(GROUPS - 1)

@@ -24,8 +24,8 @@ GROUP_COLS = GROUP_HEADS * HEAD
 WIDE = 256
 PIECES = ((0, WIDE), (WIDE, GROUP_COLS))
 VECTOR_GROUPS = 2
-BIAS_ROWS = HEADS * HEAD // (2 * P)
-BANK_ROWS = 4
+BIAS_RUNS = HEADS * HEAD // (2 * P)
+BANK_RUNS = 4
 
 FLOPS = 2 * P * HID * HEADS * HEAD
 
@@ -42,21 +42,24 @@ def tile_gptossmlaattention_pb_s_kernel(tc, hidden_states, cos, sin, Wq, bq, out
 
         hs = keep.tile([P, HID], BF16)
         nc.sync.dma_start(out=hs[:], in_=hidden_states.rearrange("b s k -> (b s) k"))
+        bias_cols = keep.tile([P, BIAS_RUNS, 2], BF16)
+        nc.sync.dma_start(out=bias_cols[:], in_=bq.rearrange("(r p e) -> p r e", p=P, e=2))
         w_rows = Wq.rearrange("(p j) n -> p j n", j=PACK)
         w_raw = []
-        for g in range(GROUPS):
+
+        def load_group(g):
             raw = per_group.tile([P, PACK, GROUP_COLS], BF16, name="raw")
             nc.sync.dma_start(out=raw[:], in_=w_rows[:, :, g * GROUP_COLS : (g + 1) * GROUP_COLS])
             w_raw.append(raw)
-        bias_rows = keep.tile([P, 2 * P], BF16)
-        nc.vector.memset(bias_rows[:], 0.0)
-        nc.scalar.dma_start(out=bias_rows[0:BIAS_ROWS, :], in_=bq.rearrange("(r c) -> r c", c=2 * P))
-        cos_sb = keep.tile([P, ROPE], BF16)
-        nc.scalar.dma_start(out=cos_sb[:], in_=cos.rearrange("b s d -> (b s) d"))
+
+        load_group(0)
+        tables = keep.tile([P, 2, ROPE], BF16)
         sin_rows = sin.rearrange("b s d -> (b s) d")
-        sin_swapped = keep.tile([P, ROPE], BF16)
-        nc.scalar.dma_start(out=sin_swapped[:, 0:HALF], in_=sin_rows[:, HALF:ROPE])
-        nc.scalar.dma_start(out=sin_swapped[:, HALF:ROPE], in_=sin_rows[:, 0:HALF])
+        nc.sync.dma_start(out=tables[:, 0, :], in_=cos.rearrange("b s d -> (b s) d"))
+        nc.sync.dma_start(out=tables[:, 1, 0:HALF], in_=sin_rows[:, HALF:ROPE])
+        nc.sync.dma_start(out=tables[:, 1, HALF:ROPE], in_=sin_rows[:, 0:HALF])
+        for g in range(1, GROUPS):
+            load_group(g)
 
         identity = keep.tile([P, P], F32)
         make_identity(nc, identity[:])
@@ -65,38 +68,34 @@ def tile_gptossmlaattention_pb_s_kernel(tc, hidden_states, cos, sin, Wq, bq, out
         for u in range(2):
             nc.tensor.transpose(hs_turned[:, u, :], hs_words[:, u, :], identity[:])
         hs_grouped = keep.tile([P, P * PACK], BF16, align_bytes=64)
-        nc.scalar.copy(
+        nc.vector.tensor_copy(
             out=hs_grouped[:].bitcast(F32).rearrange("p (s u) -> p s u", u=2),
             in_=hs_turned[:].rearrange("p u s -> p s u"),
         )
 
-        bias_turned = psum_turn.tile([P, P], F32)
-        nc.tensor.transpose(bias_turned[:], bias_rows[:].bitcast(F32), identity[:])
-        bias_cols = keep.tile([P, BIAS_ROWS], F32)
-        nc.vector.tensor_copy(out=bias_cols[:], in_=bias_turned[:, 0:BIAS_ROWS])
+        bias_words = bias_cols[:].rearrange("p r e -> p (r e)").bitcast(F32)
         bias_banks = []
-        for first_row in range(0, BIAS_ROWS, BANK_ROWS):
-            rows = min(BANK_ROWS, BIAS_ROWS - first_row)
-            spread = psum_bias.tile([P, BANK_ROWS, P], F32, name="spread")
-            for r in range(rows):
-                column = bias_cols[:, first_row + r : first_row + r + 1]
+        for first_run in range(0, BIAS_RUNS, BANK_RUNS):
+            runs = min(BANK_RUNS, BIAS_RUNS - first_run)
+            spread = psum_bias.tile([P, BANK_RUNS, P], F32, name="spread")
+            for r in range(runs):
+                column = bias_words[:, first_run + r : first_run + r + 1]
                 nc.tensor.transpose(spread[:, r, :], column.to_broadcast([P, P]), identity[:])
-            bias_banks.append((first_row, rows, spread))
+            bias_banks.append((first_run, runs, spread))
         bias = keep.tile([P, HEADS * HEAD], BF16)
 
         def copy_bias_out():
-            for first_row, rows, spread in bias_banks:
+            for first_run, runs, spread in bias_banks:
                 nc.scalar.copy(
-                    out=bias[:].bitcast(F32)[:, first_row * P : (first_row + rows) * P],
-                    in_=spread[:, 0:rows, :].rearrange("p r c -> p (r c)"),
+                    out=bias[:].bitcast(F32)[:, first_run * P : (first_run + runs) * P],
+                    in_=spread[:, 0:runs, :].rearrange("p r c -> p (r c)"),
                 )
 
         w_grouped = []
         accs = []
         qs = []
         products = []
-        cos_heads = cos_sb[:].unsqueeze(1).to_broadcast([P, GROUP_HEADS, ROPE])
-        sin_heads = sin_swapped[:].unsqueeze(1).to_broadcast([P, GROUP_HEADS, ROPE])
+        tables_heads = tables[:].unsqueeze(1).to_broadcast([P, GROUP_HEADS, 2, ROPE])
         out_rows = out.rearrange("b h s d -> s (b h) d")
 
         def regroup(g):
@@ -144,15 +143,14 @@ def tile_gptossmlaattention_pb_s_kernel(tc, hidden_states, cos, sin, Wq, bq, out
             qs.append(q)
 
         def multiply_by_tables(g):
-            by_cos = per_group.tile([P, GROUP_HEADS, ROPE], F32, name="by_cos")
-            by_sin = per_group.tile([P, GROUP_HEADS, ROPE], F32, name="by_sin")
-            x = qs[g][:, :, NOPE:HEAD]
-            nc.vector.tensor_tensor(out=by_cos[:], in0=x, in1=cos_heads, op=ALU.mult)
-            nc.vector.tensor_tensor(out=by_sin[:], in0=x, in1=sin_heads, op=ALU.mult)
-            products.append((by_cos, by_sin))
+            by_table = per_group.tile([P, GROUP_HEADS, 2, ROPE], F32, name="by_table")
+            x = qs[g][:, :, NOPE:HEAD].unsqueeze(2).to_broadcast([P, GROUP_HEADS, 2, ROPE])
+            nc.vector.tensor_tensor(out=by_table[:], in0=x, in1=tables_heads, op=ALU.mult)
+            products.append(by_table)
 
         def combine_and_store(g):
-            by_cos, by_sin = products[g]
+            by_cos = products[g][:, :, 0, :]
+            by_sin = products[g][:, :, 1, :]
             nc.vector.tensor_tensor(
                 out=qs[g][:, :, NOPE : NOPE + HALF],
                 in0=by_cos[:, :, 0:HALF],

@@ -24,8 +24,7 @@ GROUP_COLS = GROUP_HEADS * HEAD
 WIDE = 256
 PIECES = ((0, WIDE), (WIDE, GROUP_COLS))
 VECTOR_GROUPS = 2
-BIAS_RUNS = HEADS * HEAD // (2 * P)
-BANK_RUNS = 4
+BIAS_RUNS = HEADS * HEAD // HID
 
 FLOPS = 2 * P * HID * HEADS * HEAD
 
@@ -37,13 +36,13 @@ def tile_gptossmlaattention_pb_s_kernel(tc, hidden_states, cos, sin, Wq, bq, out
         keep = ctx.enter_context(tc.tile_pool(name="keep", bufs=1))
         per_group = ctx.enter_context(tc.tile_pool(name="per_group", bufs=GROUPS))
         psum_turn = ctx.enter_context(tc.psum_pool(name="psum_turn", bufs=1))
-        psum_bias = ctx.enter_context(tc.psum_pool(name="psum_bias", bufs=2))
+        psum_bias = ctx.enter_context(tc.psum_pool(name="psum_bias", bufs=BIAS_RUNS))
         psum_q = ctx.enter_context(tc.psum_pool(name="psum_q", bufs=GROUPS))
 
         hs = keep.tile([P, HID], BF16)
         nc.sync.dma_start(out=hs[:], in_=hidden_states.rearrange("b s k -> (b s) k"))
-        bias_cols = keep.tile([P, BIAS_RUNS, 2], BF16)
-        nc.sync.dma_start(out=bias_cols[:], in_=bq.rearrange("(r p e) -> p r e", p=P, e=2))
+        bias_cols = keep.tile([P, BIAS_RUNS, PACK], BF16)
+        nc.sync.dma_start(out=bias_cols[:], in_=bq.rearrange("(r p e) -> p r e", p=P, e=PACK))
         w_rows = Wq.rearrange("(p j) n -> p j n", j=PACK)
         w_raw = []
 
@@ -53,12 +52,13 @@ def tile_gptossmlaattention_pb_s_kernel(tc, hidden_states, cos, sin, Wq, bq, out
             w_raw.append(raw)
 
         load_group(0)
+        load_group(1)
         tables = keep.tile([P, 2, ROPE], BF16)
         sin_rows = sin.rearrange("b s d -> (b s) d")
         nc.sync.dma_start(out=tables[:, 0, :], in_=cos.rearrange("b s d -> (b s) d"))
         nc.sync.dma_start(out=tables[:, 1, 0:HALF], in_=sin_rows[:, HALF:ROPE])
         nc.sync.dma_start(out=tables[:, 1, HALF:ROPE], in_=sin_rows[:, 0:HALF])
-        for g in range(1, GROUPS):
+        for g in range(2, GROUPS):
             load_group(g)
 
         identity = keep.tile([P, P], F32)
@@ -73,22 +73,23 @@ def tile_gptossmlaattention_pb_s_kernel(tc, hidden_states, cos, sin, Wq, bq, out
             in_=hs_turned[:].rearrange("p u s -> p s u"),
         )
 
-        bias_words = bias_cols[:].rearrange("p r e -> p (r e)").bitcast(F32)
-        bias_banks = []
-        for first_run in range(0, BIAS_RUNS, BANK_RUNS):
-            runs = min(BANK_RUNS, BIAS_RUNS - first_run)
-            spread = psum_bias.tile([P, BANK_RUNS, P], F32, name="spread")
-            for r in range(runs):
-                column = bias_words[:, first_run + r : first_run + r + 1]
-                nc.tensor.transpose(spread[:, r, :], column.to_broadcast([P, P]), identity[:])
-            bias_banks.append((first_run, runs, spread))
+        bias_col_words = bias_cols[:].rearrange("p r e -> p (r e)").bitcast(F32)
+        bias_spread = []
+        for r in range(BIAS_RUNS):
+            spread = psum_bias.tile([P, 2, P], F32, name="spread")
+            for u in range(2):
+                word = bias_col_words[:, 2 * r + u : 2 * r + u + 1]
+                nc.tensor.transpose(spread[:, u, :], word.to_broadcast([P, P]), identity[:])
+            bias_spread.append(spread)
         bias = keep.tile([P, HEADS * HEAD], BF16)
 
         def copy_bias_out():
-            for first_run, runs, spread in bias_banks:
+            for r in range(BIAS_RUNS):
                 nc.scalar.copy(
-                    out=bias[:].bitcast(F32)[:, first_run * P : (first_run + runs) * P],
-                    in_=spread[:, 0:runs, :].rearrange("p r c -> p (r c)"),
+                    out=bias[:, r * HID : (r + 1) * HID].bitcast(F32).rearrange(
+                        "p (c u) -> p c u", u=2
+                    ),
+                    in_=bias_spread[r][:].rearrange("p u c -> p c u"),
                 )
 
         w_grouped = []

@@ -51,15 +51,14 @@ def tile_gptossmlaattention_pb_s_kernel(tc, hidden_states, cos, sin, Wq, bq, out
             nc.sync.dma_start(out=raw[:], in_=w_rows[:, :, g * GROUP_COLS : (g + 1) * GROUP_COLS])
             w_raw.append(raw)
 
-        load_group(0)
-        load_group(1)
+        for g in range(GROUPS - 1):
+            load_group(g)
         tables = keep.tile([P, 2, ROPE], BF16)
         sin_rows = sin.rearrange("b s d -> (b s) d")
         nc.sync.dma_start(out=tables[:, 0, :], in_=cos.rearrange("b s d -> (b s) d"))
         nc.sync.dma_start(out=tables[:, 1, 0:HALF], in_=sin_rows[:, HALF:ROPE])
         nc.sync.dma_start(out=tables[:, 1, HALF:ROPE], in_=sin_rows[:, 0:HALF])
-        for g in range(2, GROUPS):
-            load_group(g)
+        load_group(GROUPS - 1)
 
         identity = keep.tile([P, P], F32)
         make_identity(nc, identity[:])
@@ -178,9 +177,9 @@ def tile_gptossmlaattention_pb_s_kernel(tc, hidden_states, cos, sin, Wq, bq, out
             regroup(g)
         for g in range(GROUPS):
             add_bias(g)
-            if g > 0:
-                combine_and_store(g - 1)
             if g + 1 < GROUPS:
                 project(g + 1)
+            if g > 0:
+                combine_and_store(g - 1)
             multiply_by_tables(g)
         combine_and_store(GROUPS - 1)

@@ -9,6 +9,7 @@ U32 = mybir.dt.uint32
 U8 = mybir.dt.uint8
 FP8X4 = mybir.dt.float8_e4m3fn_x4
 ALU = mybir.AluOpType
+ACT = mybir.ActivationFunctionType
 
 P = 128
 PACK = 4
@@ -21,10 +22,9 @@ HEAD = NOPE + ROPE
 GROUP_HEADS = 2
 GROUPS = HEADS // GROUP_HEADS
 GROUP_COLS = GROUP_HEADS * HEAD
-WIDE = 256
-PIECES = ((0, WIDE), (WIDE, GROUP_COLS))
-VECTOR_GROUPS = 2
-BIAS_RUNS = HEADS * HEAD // HID
+ROPE_COLS = GROUP_HEADS * ROPE
+NOPE_COLS = GROUP_HEADS * NOPE
+SCALAR_ROPE = ((3, 1),)
 
 FLOPS = 2 * P * HID * HEADS * HEAD
 
@@ -35,151 +35,238 @@ def tile_gptossmlaattention_pb_s_kernel(tc, hidden_states, cos, sin, Wq, bq, out
         ctx.enter_context(tc.manual_schedule())
         keep = ctx.enter_context(tc.tile_pool(name="keep", bufs=1))
         per_group = ctx.enter_context(tc.tile_pool(name="per_group", bufs=GROUPS))
-        psum_turn = ctx.enter_context(tc.psum_pool(name="psum_turn", bufs=1))
-        psum_bias = ctx.enter_context(tc.psum_pool(name="psum_bias", bufs=BIAS_RUNS))
-        psum_q = ctx.enter_context(tc.psum_pool(name="psum_q", bufs=GROUPS))
+        per_head = ctx.enter_context(tc.tile_pool(name="per_head", bufs=HEADS))
+        psum_rope = ctx.enter_context(tc.psum_pool(name="psum_rope", bufs=2))
+        psum_nope = ctx.enter_context(tc.psum_pool(name="psum_nope", bufs=2))
+        psum_turn = ctx.enter_context(tc.psum_pool(name="psum_turn", bufs=4))
 
-        hs = keep.tile([P, HID], BF16)
-        nc.sync.dma_start(out=hs[:], in_=hidden_states.rearrange("b s k -> (b s) k"))
-        bias_cols = keep.tile([P, BIAS_RUNS, PACK], BF16)
-        nc.sync.dma_start(out=bias_cols[:], in_=bq.rearrange("(r p e) -> p r e", p=P, e=PACK))
+        two_identities = keep.tile([P, 2 * P], F32)
+        make_identity(nc, two_identities[:, 0:P])
+        identity = two_identities[:, 0:P]
+        exchange = two_identities[:, HALF : HALF + P]
+        bias_rows = keep.tile([P, P], BF16)
+        nc.vector.memset(bias_rows[:].bitcast(F32), 0.0)
+        nc.vector.tensor_copy(out=two_identities[:, P : 2 * P], in_=identity)
+        identity_bf = keep.tile([P, P], BF16)
+        nc.vector.tensor_copy(out=identity_bf[:], in_=identity)
+
         w_rows = Wq.rearrange("(p j) n -> p j n", j=PACK)
         w_raw = []
 
-        def load_group(g):
+        def load_columns(g, first, last):
+            nc.sync.dma_start(
+                out=w_raw[g][:, :, first:last],
+                in_=w_rows[:, :, g * GROUP_COLS + first : g * GROUP_COLS + last],
+            )
+
+        for g in range(GROUPS):
             raw = per_group.tile([P, PACK, GROUP_COLS], BF16, name="raw")
-            nc.sync.dma_start(out=raw[:], in_=w_rows[:, :, g * GROUP_COLS : (g + 1) * GROUP_COLS])
             w_raw.append(raw)
-
-        for g in range(GROUPS - 1):
-            load_group(g)
-        tables = keep.tile([P, 2, ROPE], BF16)
-        sin_rows = sin.rearrange("b s d -> (b s) d")
-        nc.sync.dma_start(out=tables[:, 0, :], in_=cos.rearrange("b s d -> (b s) d"))
-        nc.sync.dma_start(out=tables[:, 1, 0:HALF], in_=sin_rows[:, HALF:ROPE])
-        nc.sync.dma_start(out=tables[:, 1, HALF:ROPE], in_=sin_rows[:, 0:HALF])
-        load_group(GROUPS - 1)
-
-        identity = keep.tile([P, P], F32)
-        make_identity(nc, identity[:])
-        hs_words = hs[:].bitcast(F32).rearrange("s (p u) -> s u p", u=2)
-        hs_turned = psum_turn.tile([P, 2, P], F32)
-        for u in range(2):
-            nc.tensor.transpose(hs_turned[:, u, :], hs_words[:, u, :], identity[:])
-        hs_grouped = keep.tile([P, P * PACK], BF16, align_bytes=64)
-        nc.vector.tensor_copy(
-            out=hs_grouped[:].bitcast(F32).rearrange("p (s u) -> p s u", u=2),
-            in_=hs_turned[:].rearrange("p u s -> p s u"),
+        hs = keep.tile([P, HID], BF16)
+        nc.sync.dma_start(out=hs[:], in_=hidden_states.rearrange("b s k -> (b s) k"))
+        load_columns(0, 0, GROUP_COLS)
+        nc.sync.dma_start(
+            out=bias_rows[0:HEADS, :], in_=bq.rearrange("(h d) -> h d", d=HEAD)[:, NOPE:HEAD]
         )
+        nc.sync.dma_start(
+            out=bias_rows[HEADS : HEADS + GROUPS, :].rearrange("g (h d) -> g h d", d=NOPE),
+            in_=bq.rearrange("(g h d) -> g h d", h=GROUP_HEADS, d=HEAD)[:, :, 0:NOPE],
+        )
+        tables = keep.tile([P, 2, ROPE], BF16)
+        sin_rows = keep.tile([P, ROPE], BF16)
+        nc.sync.dma_start(out=tables[:, 0, :], in_=cos.rearrange("b s d -> (b s) d"))
+        nc.sync.dma_start(out=sin_rows[:], in_=sin.rearrange("b s d -> (b s) d"))
+        nc.gpsimd.tensor_scalar(
+            out=tables[:, 1, 0:HALF], in0=sin_rows[:, HALF:ROPE],
+            scalar1=1.0, scalar2=0.0, op0=ALU.mult, op1=ALU.add,
+        )
+        nc.gpsimd.tensor_scalar(
+            out=tables[:, 1, HALF:ROPE], in0=sin_rows[:, 0:HALF],
+            scalar1=-1.0, scalar2=0.0, op0=ALU.mult, op1=ALU.add,
+        )
+        for g in range(1, GROUPS):
+            load_columns(g, 0, GROUP_COLS)
 
-        bias_col_words = bias_cols[:].rearrange("p r e -> p (r e)").bitcast(F32)
-        bias_spread = []
-        for r in range(BIAS_RUNS):
-            spread = psum_bias.tile([P, 2, P], F32, name="spread")
+        hs_words = hs[:].bitcast(F32).rearrange("s (p u) -> s u p", u=2)
+        hs_grouped = keep.tile([P, P * PACK], BF16, align_bytes=64)
+
+        def turn_hidden_states():
+            hs_turned = psum_turn.tile([P, 2, P], F32, name="back")
             for u in range(2):
-                word = bias_col_words[:, 2 * r + u : 2 * r + u + 1]
-                nc.tensor.transpose(spread[:, u, :], word.to_broadcast([P, P]), identity[:])
-            bias_spread.append(spread)
-        bias = keep.tile([P, HEADS * HEAD], BF16)
-
-        def copy_bias_out():
-            for r in range(BIAS_RUNS):
-                nc.scalar.copy(
-                    out=bias[:, r * HID : (r + 1) * HID].bitcast(F32).rearrange(
-                        "p (c u) -> p c u", u=2
-                    ),
-                    in_=bias_spread[r][:].rearrange("p u c -> p c u"),
-                )
+                nc.tensor.transpose(hs_turned[:, u, :], hs_words[:, u, :], identity)
+            nc.scalar.copy(
+                out=hs_grouped[:].bitcast(F32).rearrange("p (s u) -> p s u", u=2),
+                in_=hs_turned[:].rearrange("p u s -> p s u"),
+            )
 
         w_grouped = []
-        accs = []
-        qs = []
-        products = []
-        tables_heads = tables[:].unsqueeze(1).to_broadcast([P, GROUP_HEADS, 2, ROPE])
+        w_codes = []
+        w_scales = []
+        accs_rope = []
+        accs_nope = []
+        rope_place = {}
+        nope_place = {}
         out_rows = out.rearrange("b h s d -> s (b h) d")
 
-        def regroup(g):
+        def regroup_piece(copy, g, first_out, first_in, cols):
+            copy(
+                out=w_grouped[g][:, PACK * first_out : PACK * (first_out + cols)].rearrange(
+                    "p (c i j) -> p c j i", i=4, j=PACK
+                ),
+                in_=w_raw[g][:, :, first_in : first_in + cols].rearrange(
+                    "p j (c i) -> p c j i", i=4
+                ),
+            )
+
+        def new_grouped():
             grouped = per_group.tile([P, GROUP_COLS * PACK], BF16, align_bytes=64, name="grouped")
-            for first, last in PIECES:
-                by_vector = g < VECTOR_GROUPS and first == 0
-                copy = nc.vector.tensor_copy if by_vector else nc.scalar.copy
-                copy(
-                    out=grouped[:, PACK * first : PACK * last].rearrange(
-                        "p (c i j) -> p c j i", i=4, j=PACK
-                    ),
-                    in_=w_raw[g][:, :, first:last].rearrange("p j (c i) -> p c j i", i=4),
-                )
             w_grouped.append(grouped)
 
-        def project(g):
+        def regroup_rope(g, h):
+            by_scalar = (g, h) in SCALAR_ROPE
+            copy = nc.scalar.copy if by_scalar else nc.vector.tensor_copy
+            regroup_piece(copy, g, h * ROPE, h * HEAD + NOPE, ROPE)
+
+        def regroup(g):
+            new_grouped()
+            for h in range(GROUP_HEADS):
+                regroup_rope(g, h)
+            for h in range(GROUP_HEADS):
+                regroup_piece(nc.scalar.copy, g, ROPE_COLS + h * NOPE, h * HEAD, NOPE)
+
+        def new_codes():
             codes = per_group.tile([P, GROUP_COLS], U32, align_bytes=64, name="codes")
             scales = per_group.tile([P, GROUP_COLS], U8, align_bytes=64, name="scales")
-            acc = psum_q.tile([P, GROUP_COLS], F32, name="acc")
-            for first, last in PIECES:
-                nc.vector.quantize_mx(
-                    out=codes[:, first:last].bitcast(FP8X4),
-                    scales=scales[:, first:last],
-                    in_=w_grouped[g][:, PACK * first : PACK * last],
-                )
-                nc.tensor.matmul_mx(
-                    out=acc[:, first:last],
-                    lhsT=hs_codes[:].bitcast(FP8X4),
-                    lhsT_scale=hs_scales[:],
-                    rhs=codes[:, first:last].bitcast(FP8X4),
-                    rhs_scale=scales[:, first:last],
-                    start=True,
-                    stop=True,
-                )
-            accs.append(acc)
+            w_codes.append(codes)
+            w_scales.append(scales)
 
-        def add_bias(g):
-            q = per_group.tile([P, GROUP_HEADS, HEAD], F32, name="q")
-            nc.vector.tensor_tensor(
-                out=q[:].rearrange("p h d -> p (h d)"),
-                in0=accs[g][:],
-                in1=bias[:, g * GROUP_COLS : (g + 1) * GROUP_COLS],
-                op=ALU.add,
+        def quantise(g, first, last):
+            nc.vector.quantize_mx(
+                out=w_codes[g][:, first:last].bitcast(FP8X4),
+                scales=w_scales[g][:, first:last],
+                in_=w_grouped[g][:, PACK * first : PACK * last],
             )
-            qs.append(q)
 
-        def multiply_by_tables(g):
-            by_table = per_group.tile([P, GROUP_HEADS, 2, ROPE], F32, name="by_table")
-            x = qs[g][:, :, NOPE:HEAD].unsqueeze(2).to_broadcast([P, GROUP_HEADS, 2, ROPE])
-            nc.vector.tensor_tensor(out=by_table[:], in0=x, in1=tables_heads, op=ALU.mult)
-            products.append(by_table)
+        def multiply(g, acc, first):
+            nc.tensor.matmul_mx(
+                out=acc,
+                lhsT=w_codes[g][:, first : first + P].bitcast(FP8X4),
+                lhsT_scale=w_scales[g][:, first : first + P],
+                rhs=hs_codes[:].bitcast(FP8X4),
+                rhs_scale=hs_scales[:],
+                start=True,
+                stop=True,
+            )
 
-        def combine_and_store(g):
-            by_cos = products[g][:, :, 0, :]
-            by_sin = products[g][:, :, 1, :]
-            nc.vector.tensor_tensor(
-                out=qs[g][:, :, NOPE : NOPE + HALF],
-                in0=by_cos[:, :, 0:HALF],
-                in1=by_sin[:, :, HALF:ROPE],
-                op=ALU.subtract,
+        def project_rope(g):
+            new_codes()
+            acc_rope = psum_rope.tile([P, GROUP_HEADS, P], F32, name="acc_rope")
+            accs_rope.append(acc_rope)
+            quantise(g, 0, ROPE_COLS)
+            for h in range(GROUP_HEADS):
+                multiply(g, acc_rope[:, h, :], h * ROPE)
+
+        def project_nope(g):
+            acc_nope = psum_nope.tile([P, P], F32, name="acc_nope")
+            accs_nope.append(acc_nope)
+            quantise(g, ROPE_COLS, GROUP_COLS)
+            multiply(g, acc_nope[:], ROPE_COLS)
+
+        def rotate(g, h):
+            head = g * GROUP_HEADS + h
+            by_table = per_head.tile([P, 2, P], F32, name="by_table")
+            nc.vector.scalar_tensor_tensor(
+                out=by_table[:],
+                in0=accs_rope[g][:, h, :].unsqueeze(1).to_broadcast([P, 2, P]),
+                scalar=bias_cols[:, head : head + 1],
+                in1=tables_turned[:],
+                op0=ALU.add,
+                op1=ALU.mult,
             )
-            nc.vector.tensor_tensor(
-                out=qs[g][:, :, NOPE + HALF : HEAD],
-                in0=by_cos[:, :, HALF:ROPE],
-                in1=by_sin[:, :, 0:HALF],
-                op=ALU.add,
+            place = rope_place[(g, h)]
+            nc.tensor.matmul(
+                out=place, lhsT=by_table[:, 0, :], rhs=identity,
+                start=True, stop=False, is_transpose=True,
             )
+            nc.tensor.matmul(
+                out=place, lhsT=by_table[:, 1, :], rhs=exchange,
+                start=False, stop=True, is_transpose=True,
+            )
+
+        def shift_nope(g):
+            plain = per_group.tile([P, P], F32, name="plain")
+            nc.scalar.activation(
+                out=plain[:], in_=accs_nope[g][:], func=ACT.Identity,
+                bias=bias_cols[:, HEADS + g : HEADS + g + 1], scale=1.0,
+            )
+            nc.tensor.transpose(nope_place[g], plain[:], identity)
+
+        def new_bank(g, heads, with_nope):
+            back = psum_turn.tile([P, GROUP_COLS], F32, name="back")
+            for i, h in enumerate(heads):
+                rope_place[(g, h)] = back[:, i * ROPE : (i + 1) * ROPE]
+            if with_nope:
+                nope_place[g] = back[:, len(heads) * ROPE : len(heads) * ROPE + NOPE_COLS]
+            return back
+
+        def store(copy, back, g, heads, with_nope):
+            rope_cols = len(heads) * ROPE
+            cols = rope_cols + (NOPE_COLS if with_nope else 0)
+            q = per_head.tile([P, GROUP_COLS], F32, name="q")
+            copy(out=q[:, 0:cols], in_=back[:, 0:cols])
+            first = g * GROUP_HEADS
             nc.sync.dma_start(
-                out=out_rows[:, g * GROUP_HEADS : (g + 1) * GROUP_HEADS, :], in_=qs[g][:]
+                out=out_rows[:, first + heads[0] : first + heads[0] + len(heads), NOPE:HEAD],
+                in_=q[:, 0:rope_cols].rearrange("p (h d) -> p h d", d=ROPE),
             )
+            if with_nope:
+                nc.sync.dma_start(
+                    out=out_rows[:, first : first + GROUP_HEADS, 0:NOPE],
+                    in_=q[:, rope_cols:cols].rearrange("p (h d) -> p h d", d=NOPE),
+                )
 
+        def keep_tensor_engine_busy(times):
+            for i in range(times):
+                nc.tensor.transpose(idle_work[:, 0:P], identity, identity)
+
+        idle_work = psum_turn.tile([P, GROUP_COLS], F32, name="back")
+        keep_tensor_engine_busy(9)
+        turn_hidden_states()
+        keep_tensor_engine_busy(6)
         regroup(0)
-        copy_bias_out()
+        consts_turned = psum_turn.tile([P, 3, P], BF16, name="back")
+        for t in range(2):
+            nc.tensor.transpose(consts_turned[:, t, :], tables[:, t, :], identity_bf[:])
+        nc.tensor.transpose(consts_turned[:, 2, :], bias_rows[:], identity_bf[:])
+        tables_turned = keep.tile([P, 2, P], BF16)
+        nc.scalar.copy(out=tables_turned[:], in_=consts_turned[:, 0:2, :])
+        bias_cols = keep.tile([P, HEADS + GROUPS], F32)
+        nc.scalar.copy(out=bias_cols[:], in_=consts_turned[:, 2, 0 : HEADS + GROUPS])
         hs_codes = keep.tile([P, P], U32, align_bytes=64)
         hs_scales = keep.tile([P, P], U8, align_bytes=64)
         nc.vector.quantize_mx(out=hs_codes[:].bitcast(FP8X4), scales=hs_scales[:], in_=hs_grouped[:])
-        project(0)
-        for g in range(1, GROUPS):
-            regroup(g)
-        for g in range(GROUPS):
-            add_bias(g)
-            if g + 1 < GROUPS:
-                project(g + 1)
+        project_rope(0)
+        project_nope(0)
+        regroup(1)
+        both = (0, 1)
+        banks = []
+        for g in range(GROUPS - 1):
+            banks.append(new_bank(g, both, True))
+            rotate(g, 0)
+            project_rope(g + 1)
+            shift_nope(g)
+            project_nope(g + 1)
+            rotate(g, 1)
+            if g + 2 < GROUPS:
+                regroup(g + 2)
             if g > 0:
-                combine_and_store(g - 1)
-            multiply_by_tables(g)
-        combine_and_store(GROUPS - 1)
+                store(nc.scalar.copy, banks[g - 1], g - 1, both, True)
+        last = GROUPS - 1
+        bank_a = new_bank(last, (0,), True)
+        bank_b = new_bank(last, (1,), False)
+        shift_nope(last)
+        rotate(last, 0)
+        rotate(last, 1)
+        store(nc.scalar.copy, banks[last - 1], last - 1, both, True)
+        store(nc.scalar.copy, bank_a, last, (0,), True)
+        store(nc.vector.tensor_copy, bank_b, last, (1,), False)

@@ -104,6 +104,8 @@ def tile_gptossmlaattention_pb_s_kernel(tc, hidden_states, cos, sin, Wq, bq, out
         w_scales = []
         accs_rope = []
         accs_nope = []
+        products = {}
+        shifted = {}
         rope_place = {}
         nope_place = {}
         out_rows = out.rearrange("b h s d -> s (b h) d")
@@ -127,10 +129,7 @@ def tile_gptossmlaattention_pb_s_kernel(tc, hidden_states, cos, sin, Wq, bq, out
             copy = nc.scalar.copy if by_scalar else nc.vector.tensor_copy
             regroup_piece(copy, g, h * ROPE, h * HEAD + NOPE, ROPE)
 
-        def regroup(g):
-            new_grouped()
-            for h in range(GROUP_HEADS):
-                regroup_rope(g, h)
+        def regroup_nope(g):
             for h in range(GROUP_HEADS):
                 regroup_piece(nc.scalar.copy, g, ROPE_COLS + h * NOPE, h * HEAD, NOPE)
 
@@ -172,7 +171,7 @@ def tile_gptossmlaattention_pb_s_kernel(tc, hidden_states, cos, sin, Wq, bq, out
             quantise(g, ROPE_COLS, GROUP_COLS)
             multiply(g, acc_nope[:], ROPE_COLS)
 
-        def rotate(g, h):
+        def multiply_by_tables(g, h):
             head = g * GROUP_HEADS + h
             by_table = per_head.tile([P, 2, P], F32, name="by_table")
             nc.vector.scalar_tensor_tensor(
@@ -183,23 +182,27 @@ def tile_gptossmlaattention_pb_s_kernel(tc, hidden_states, cos, sin, Wq, bq, out
                 op0=ALU.add,
                 op1=ALU.mult,
             )
-            place = rope_place[(g, h)]
-            nc.tensor.matmul(
-                out=place, lhsT=by_table[:, 0, :], rhs=identity,
-                start=True, stop=False, is_transpose=True,
-            )
-            nc.tensor.matmul(
-                out=place, lhsT=by_table[:, 1, :], rhs=exchange,
-                start=False, stop=True, is_transpose=True,
-            )
+            products[(g, h)] = by_table
 
-        def shift_nope(g):
+        def add_bias_to_nope(g):
             plain = per_group.tile([P, P], F32, name="plain")
             nc.scalar.activation(
                 out=plain[:], in_=accs_nope[g][:], func=ACT.Identity,
                 bias=bias_cols[:, HEADS + g : HEADS + g + 1], scale=1.0,
             )
-            nc.tensor.transpose(nope_place[g], plain[:], identity)
+            shifted[g] = plain
+
+        def turn_back(g):
+            nc.tensor.transpose(nope_place[g], shifted[g][:], identity)
+            for h in range(GROUP_HEADS):
+                nc.tensor.matmul(
+                    out=rope_place[(g, h)], lhsT=products[(g, h)][:, 0, :], rhs=identity,
+                    start=True, stop=False, is_transpose=True,
+                )
+                nc.tensor.matmul(
+                    out=rope_place[(g, h)], lhsT=products[(g, h)][:, 1, :], rhs=exchange,
+                    start=False, stop=True, is_transpose=True,
+                )
 
         def new_bank(g, heads, with_nope):
             back = psum_turn.tile([P, GROUP_COLS], F32, name="back")
@@ -233,7 +236,11 @@ def tile_gptossmlaattention_pb_s_kernel(tc, hidden_states, cos, sin, Wq, bq, out
         keep_tensor_engine_busy(9)
         turn_hidden_states()
         keep_tensor_engine_busy(6)
-        regroup(0)
+        for g in range(GROUPS):
+            new_grouped()
+        regroup_rope(0, 0)
+        regroup_rope(0, 1)
+        regroup_nope(0)
         consts_turned = psum_turn.tile([P, 3, P], BF16, name="back")
         for t in range(2):
             nc.tensor.transpose(consts_turned[:, t, :], tables[:, t, :], identity_bf[:])
@@ -245,28 +252,45 @@ def tile_gptossmlaattention_pb_s_kernel(tc, hidden_states, cos, sin, Wq, bq, out
         hs_codes = keep.tile([P, P], U32, align_bytes=64)
         hs_scales = keep.tile([P, P], U8, align_bytes=64)
         nc.vector.quantize_mx(out=hs_codes[:].bitcast(FP8X4), scales=hs_scales[:], in_=hs_grouped[:])
-        project_rope(0)
-        project_nope(0)
-        regroup(1)
         both = (0, 1)
-        banks = []
-        for g in range(GROUPS - 1):
-            banks.append(new_bank(g, both, True))
-            rotate(g, 0)
-            project_rope(g + 1)
-            shift_nope(g)
-            project_nope(g + 1)
-            rotate(g, 1)
-            if g + 2 < GROUPS:
-                regroup(g + 2)
-            if g > 0:
-                store(nc.scalar.copy, banks[g - 1], g - 1, both, True)
-        last = GROUPS - 1
-        bank_a = new_bank(last, (0,), True)
-        bank_b = new_bank(last, (1,), False)
-        shift_nope(last)
-        rotate(last, 0)
-        rotate(last, 1)
-        store(nc.scalar.copy, banks[last - 1], last - 1, both, True)
-        store(nc.scalar.copy, bank_a, last, (0,), True)
-        store(nc.vector.tensor_copy, bank_b, last, (1,), False)
+        project_rope(0)
+        regroup_rope(1, 0)
+        project_nope(0)
+        regroup_rope(1, 1)
+        regroup_nope(1)
+        multiply_by_tables(0, 0)
+        project_rope(1)
+        project_nope(1)
+        add_bias_to_nope(0)
+        regroup_nope(2)
+        multiply_by_tables(0, 1)
+        multiply_by_tables(1, 0)
+        multiply_by_tables(1, 1)
+        add_bias_to_nope(1)
+        bank_0 = new_bank(0, both, True)
+        bank_1 = new_bank(1, both, True)
+        turn_back(0)
+        turn_back(1)
+        regroup_rope(2, 0)
+        regroup_rope(2, 1)
+        regroup_rope(3, 0)
+        regroup_rope(3, 1)
+        regroup_nope(3)
+        store(nc.scalar.copy, bank_0, 0, both, True)
+        store(nc.scalar.copy, bank_1, 1, both, True)
+        project_rope(2)
+        project_nope(2)
+        project_rope(3)
+        project_nope(3)
+        for g in (2, 3):
+            multiply_by_tables(g, 0)
+            multiply_by_tables(g, 1)
+            add_bias_to_nope(g)
+        bank_2 = new_bank(2, both, True)
+        bank_3a = new_bank(3, (0,), True)
+        bank_3b = new_bank(3, (1,), False)
+        turn_back(2)
+        turn_back(3)
+        store(nc.scalar.copy, bank_2, 2, both, True)
+        store(nc.scalar.copy, bank_3a, 3, (0,), True)
+        store(nc.vector.tensor_copy, bank_3b, 3, (1,), False)

@@ -228,14 +228,7 @@ def tile_gptossmlaattention_pb_s_kernel(tc, hidden_states, cos, sin, Wq, bq, out
                     in_=q[:, rope_cols:cols].rearrange("p (h d) -> p h d", d=NOPE),
                 )
 
-        def keep_tensor_engine_busy(times):
-            for i in range(times):
-                nc.tensor.transpose(idle_work[:, 0:P], identity, identity)
-
-        idle_work = psum_turn.tile([P, GROUP_COLS], F32, name="back")
-        keep_tensor_engine_busy(9)
         turn_hidden_states()
-        keep_tensor_engine_busy(6)
         for g in range(GROUPS):
             new_grouped()
         regroup_rope(0, 0)

@@ -76,14 +76,6 @@ def tile_gptossmlaattention_pb_s_kernel(tc, hidden_states, cos, sin, Wq, bq, out
         sin_rows = keep.tile([P, ROPE], BF16)
         nc.sync.dma_start(out=tables[:, 0, :], in_=cos.rearrange("b s d -> (b s) d"))
         nc.sync.dma_start(out=sin_rows[:], in_=sin.rearrange("b s d -> (b s) d"))
-        nc.gpsimd.tensor_scalar(
-            out=tables[:, 1, 0:HALF], in0=sin_rows[:, HALF:ROPE],
-            scalar1=1.0, scalar2=0.0, op0=ALU.mult, op1=ALU.add,
-        )
-        nc.gpsimd.tensor_scalar(
-            out=tables[:, 1, HALF:ROPE], in0=sin_rows[:, 0:HALF],
-            scalar1=-1.0, scalar2=0.0, op0=ALU.mult, op1=ALU.add,
-        )
         for g in range(1, GROUPS):
             load_columns(g, 0, GROUP_COLS)
 
@@ -229,6 +221,10 @@ def tile_gptossmlaattention_pb_s_kernel(tc, hidden_states, cos, sin, Wq, bq, out
                 )
 
         turn_hidden_states()
+        nc.scalar.copy(out=tables[:, 1, 0:HALF], in_=sin_rows[:, HALF:ROPE])
+        nc.scalar.activation(
+            out=tables[:, 1, HALF:ROPE], in_=sin_rows[:, 0:HALF], func=ACT.Copy, scale=-1.0
+        )
         for g in range(GROUPS):
             new_grouped()
         regroup_rope(0, 0)

@@ -244,12 +244,12 @@ def tile_gptossmlaattention_pb_s_kernel(tc, hidden_states, cos, sin, Wq, bq, out
         both = (0, 1)
         project_rope(0)
         regroup_rope(1, 0)
-        project_nope(0)
         regroup_rope(1, 1)
+        project_nope(0)
         regroup_nope(1)
-        multiply_by_tables(0, 0)
         project_rope(1)
         project_nope(1)
+        multiply_by_tables(0, 0)
         add_bias_to_nope(0)
         regroup_nope(2)
         multiply_by_tables(0, 1)

@@ -185,7 +185,11 @@ def tile_gptossmlaattention_pb_s_kernel(tc, hidden_states, cos, sin, Wq, bq, out
             shifted[g] = plain
 
         def turn_back(g):
-            nc.tensor.transpose(nope_place[g], shifted[g][:], identity)
+            nc.tensor.matmul(
+                out=nope_place[g], lhsT=shifted[g][:],
+                rhs=identity.rearrange("p (h d) -> p h d", h=GROUP_HEADS),
+                start=True, stop=True, is_transpose=True,
+            )
             for h in range(GROUP_HEADS):
                 nc.tensor.matmul(
                     out=rope_place[(g, h)], lhsT=products[(g, h)][:, 0, :], rhs=identity,
@@ -196,29 +200,23 @@ def tile_gptossmlaattention_pb_s_kernel(tc, hidden_states, cos, sin, Wq, bq, out
                     start=False, stop=True, is_transpose=True,
                 )
 
-        def new_bank(g, heads, with_nope):
-            back = psum_turn.tile([P, GROUP_COLS], F32, name="back")
-            for i, h in enumerate(heads):
-                rope_place[(g, h)] = back[:, i * ROPE : (i + 1) * ROPE]
-            if with_nope:
-                nope_place[g] = back[:, len(heads) * ROPE : len(heads) * ROPE + NOPE_COLS]
+        def new_bank(g):
+            back = psum_turn.tile([P, GROUP_HEADS, HEAD], F32, name="back")
+            for h in range(GROUP_HEADS):
+                rope_place[(g, h)] = back[:, h, NOPE:HEAD]
+            nope_place[g] = back[:, :, 0:NOPE]
             return back
 
-        def store(copy, back, g, heads, with_nope):
-            rope_cols = len(heads) * ROPE
-            cols = rope_cols + (NOPE_COLS if with_nope else 0)
-            q = per_head.tile([P, GROUP_COLS], F32, name="q")
-            copy(out=q[:, 0:cols], in_=back[:, 0:cols])
-            first = g * GROUP_HEADS
+        def send(q, g, first_head, heads):
             nc.sync.dma_start(
-                out=out_rows[:, first + heads[0] : first + heads[0] + len(heads), NOPE:HEAD],
-                in_=q[:, 0:rope_cols].rearrange("p (h d) -> p h d", d=ROPE),
+                out=out_rows[:, g * GROUP_HEADS + first_head : g * GROUP_HEADS + first_head + heads, :],
+                in_=q[:, first_head : first_head + heads, :],
             )
-            if with_nope:
-                nc.sync.dma_start(
-                    out=out_rows[:, first : first + GROUP_HEADS, 0:NOPE],
-                    in_=q[:, rope_cols:cols].rearrange("p (h d) -> p h d", d=NOPE),
-                )
+
+        def store(back, g):
+            q = per_group.tile([P, GROUP_HEADS, HEAD], F32, name="q")
+            nc.scalar.copy(out=q[:], in_=back[:])
+            send(q, g, 0, GROUP_HEADS)
 
         turn_hidden_states()
         nc.scalar.copy(out=tables[:, 1, 0:HALF], in_=sin_rows[:, HALF:ROPE])
@@ -241,7 +239,6 @@ def tile_gptossmlaattention_pb_s_kernel(tc, hidden_states, cos, sin, Wq, bq, out
         hs_codes = keep.tile([P, P], U32, align_bytes=64)
         hs_scales = keep.tile([P, P], U8, align_bytes=64)
         nc.vector.quantize_mx(out=hs_codes[:].bitcast(FP8X4), scales=hs_scales[:], in_=hs_grouped[:])
-        both = (0, 1)
         project_rope(0)
         regroup_rope(1, 0)
         regroup_rope(1, 1)
@@ -256,8 +253,8 @@ def tile_gptossmlaattention_pb_s_kernel(tc, hidden_states, cos, sin, Wq, bq, out
         multiply_by_tables(1, 0)
         multiply_by_tables(1, 1)
         add_bias_to_nope(1)
-        bank_0 = new_bank(0, both, True)
-        bank_1 = new_bank(1, both, True)
+        bank_0 = new_bank(0)
+        bank_1 = new_bank(1)
         turn_back(0)
         turn_back(1)
         regroup_rope(2, 0)
@@ -265,8 +262,8 @@ def tile_gptossmlaattention_pb_s_kernel(tc, hidden_states, cos, sin, Wq, bq, out
         regroup_rope(3, 0)
         regroup_rope(3, 1)
         regroup_nope(3)
-        store(nc.scalar.copy, bank_0, 0, both, True)
-        store(nc.scalar.copy, bank_1, 1, both, True)
+        store(bank_0, 0)
+        store(bank_1, 1)
         project_rope(2)
         project_nope(2)
         project_rope(3)
@@ -275,11 +272,17 @@ def tile_gptossmlaattention_pb_s_kernel(tc, hidden_states, cos, sin, Wq, bq, out
             multiply_by_tables(g, 0)
             multiply_by_tables(g, 1)
             add_bias_to_nope(g)
-        bank_2 = new_bank(2, both, True)
-        bank_3a = new_bank(3, (0,), True)
-        bank_3b = new_bank(3, (1,), False)
+        bank_2 = new_bank(2)
+        bank_3 = new_bank(3)
+        last_rope = psum_turn.tile([P, ROPE], F32, name="back")
+        rope_place[(3, 1)] = last_rope[:]
         turn_back(2)
         turn_back(3)
-        store(nc.scalar.copy, bank_2, 2, both, True)
-        store(nc.scalar.copy, bank_3a, 3, (0,), True)
-        store(nc.vector.tensor_copy, bank_3b, 3, (1,), False)
+        store(bank_2, 2)
+        q = per_group.tile([P, GROUP_HEADS, HEAD], F32, name="q")
+        q_cols = q[:].rearrange("p h d -> p (h d)")
+        bank_3_cols = bank_3[:].rearrange("p h d -> p (h d)")
+        nc.scalar.copy(out=q_cols[:, 0 : HEAD + NOPE], in_=bank_3_cols[:, 0 : HEAD + NOPE])
+        send(q, 3, 0, 1)
+        nc.vector.tensor_copy(out=q[:, 1, NOPE:HEAD], in_=last_rope[:])
+        send(q, 3, 1, 1)

@@ -184,21 +184,22 @@ def tile_gptossmlaattention_pb_s_kernel(tc, hidden_states, cos, sin, Wq, bq, out
             )
             shifted[g] = plain
 
-        def turn_back(g):
+        def turn_back_nope(g):
             nc.tensor.matmul(
                 out=nope_place[g], lhsT=shifted[g][:],
                 rhs=identity.rearrange("p (h d) -> p h d", h=GROUP_HEADS),
                 start=True, stop=True, is_transpose=True,
             )
-            for h in range(GROUP_HEADS):
-                nc.tensor.matmul(
-                    out=rope_place[(g, h)], lhsT=products[(g, h)][:, 0, :], rhs=identity,
-                    start=True, stop=False, is_transpose=True,
-                )
-                nc.tensor.matmul(
-                    out=rope_place[(g, h)], lhsT=products[(g, h)][:, 1, :], rhs=exchange,
-                    start=False, stop=True, is_transpose=True,
-                )
+
+        def turn_back_rope(g, h):
+            nc.tensor.matmul(
+                out=rope_place[(g, h)], lhsT=products[(g, h)][:, 0, :], rhs=identity,
+                start=True, stop=False, is_transpose=True,
+            )
+            nc.tensor.matmul(
+                out=rope_place[(g, h)], lhsT=products[(g, h)][:, 1, :], rhs=exchange,
+                start=False, stop=True, is_transpose=True,
+            )
 
         def new_bank(g):
             back = psum_turn.tile([P, GROUP_HEADS, HEAD], F32, name="back")
@@ -255,8 +256,11 @@ def tile_gptossmlaattention_pb_s_kernel(tc, hidden_states, cos, sin, Wq, bq, out
         add_bias_to_nope(1)
         bank_0 = new_bank(0)
         bank_1 = new_bank(1)
-        turn_back(0)
-        turn_back(1)
+        for g in (0, 1):
+            for h in range(GROUP_HEADS):
+                turn_back_rope(g, h)
+        for g in (0, 1):
+            turn_back_nope(g)
         regroup_rope(2, 0)
         regroup_rope(2, 1)
         regroup_rope(3, 0)
@@ -272,17 +276,23 @@ def tile_gptossmlaattention_pb_s_kernel(tc, hidden_states, cos, sin, Wq, bq, out
             multiply_by_tables(g, 0)
             multiply_by_tables(g, 1)
             add_bias_to_nope(g)
-        bank_2 = new_bank(2)
-        bank_3 = new_bank(3)
-        last_rope = psum_turn.tile([P, ROPE], F32, name="back")
-        rope_place[(3, 1)] = last_rope[:]
-        turn_back(2)
-        turn_back(3)
-        store(bank_2, 2)
-        q = per_group.tile([P, GROUP_HEADS, HEAD], F32, name="q")
-        q_cols = q[:].rearrange("p h d -> p (h d)")
-        bank_3_cols = bank_3[:].rearrange("p h d -> p (h d)")
-        nc.scalar.copy(out=q_cols[:, 0 : HEAD + NOPE], in_=bank_3_cols[:, 0 : HEAD + NOPE])
-        send(q, 3, 0, 1)
-        nc.vector.tensor_copy(out=q[:, 1, NOPE:HEAD], in_=last_rope[:])
-        send(q, 3, 1, 1)
+        wide_banks = {}
+        narrow_banks = {}
+        for g in (2, 3):
+            wide_banks[g] = new_bank(g)
+            narrow_banks[g] = psum_turn.tile([P, ROPE], F32, name="back")
+            rope_place[(g, 1)] = narrow_banks[g][:]
+        turn_back_rope(2, 0)
+        turn_back_nope(2)
+        turn_back_rope(2, 1)
+        turn_back_rope(3, 0)
+        turn_back_nope(3)
+        turn_back_rope(3, 1)
+        for g in (2, 3):
+            q = per_group.tile([P, GROUP_HEADS, HEAD], F32, name="q")
+            q_cols = q[:].rearrange("p h d -> p (h d)")
+            bank_cols = wide_banks[g][:].rearrange("p h d -> p (h d)")
+            nc.scalar.copy(out=q_cols[:, 0 : HEAD + NOPE], in_=bank_cols[:, 0 : HEAD + NOPE])
+            send(q, g, 0, 1)
+            nc.vector.tensor_copy(out=q[:, 1, NOPE:HEAD], in_=narrow_banks[g][:])
+            send(q, g, 1, 1)

@@ -24,7 +24,9 @@ GROUPS = HEADS // GROUP_HEADS
 GROUP_COLS = GROUP_HEADS * HEAD
 ROPE_COLS = GROUP_HEADS * ROPE
 NOPE_COLS = GROUP_HEADS * NOPE
-SCALAR_ROPE = ((3, 1),)
+PAIRS = 2
+PAIR_HEADS = HEADS // PAIRS
+SCALAR_ROPE = ((2, 1), (3, 1))
 
 FLOPS = 2 * P * HID * HEADS * HEAD
 
@@ -35,17 +37,22 @@ def tile_gptossmlaattention_pb_s_kernel(tc, hidden_states, cos, sin, Wq, bq, out
         ctx.enter_context(tc.manual_schedule())
         keep = ctx.enter_context(tc.tile_pool(name="keep", bufs=1))
         per_group = ctx.enter_context(tc.tile_pool(name="per_group", bufs=GROUPS))
+        per_pair = ctx.enter_context(tc.tile_pool(name="per_pair", bufs=PAIRS))
         per_head = ctx.enter_context(tc.tile_pool(name="per_head", bufs=HEADS))
         psum_rope = ctx.enter_context(tc.psum_pool(name="psum_rope", bufs=2))
-        psum_nope = ctx.enter_context(tc.psum_pool(name="psum_nope", bufs=2))
+        psum_nope = ctx.enter_context(tc.psum_pool(name="psum_nope", bufs=PAIRS))
         psum_turn = ctx.enter_context(tc.psum_pool(name="psum_turn", bufs=4))
 
         two_identities = keep.tile([P, 2 * P], F32)
         make_identity(nc, two_identities[:, 0:P])
         identity = two_identities[:, 0:P]
         exchange = two_identities[:, HALF : HALF + P]
-        bias_rows = keep.tile([P, P], BF16)
+        bias_rows = keep.tile([P, ROPE + HEADS * NOPE], BF16)
         nc.vector.memset(bias_rows[:].bitcast(F32), 0.0)
+        rope_bias_rows = bias_rows[:, 0:ROPE]
+        nope_bias_row = bias_rows[:, ROPE : ROPE + HEADS * NOPE]
+        ones = keep.tile([P, P], BF16)
+        nc.vector.memset(ones[:], 1.0)
         nc.vector.tensor_copy(out=two_identities[:, P : 2 * P], in_=identity)
         identity_bf = keep.tile([P, P], BF16)
         nc.vector.tensor_copy(out=identity_bf[:], in_=identity)
@@ -53,31 +60,28 @@ def tile_gptossmlaattention_pb_s_kernel(tc, hidden_states, cos, sin, Wq, bq, out
         w_rows = Wq.rearrange("(p j) n -> p j n", j=PACK)
         w_raw = []
 
-        def load_columns(g, first, last):
-            nc.sync.dma_start(
-                out=w_raw[g][:, :, first:last],
-                in_=w_rows[:, :, g * GROUP_COLS + first : g * GROUP_COLS + last],
-            )
-
-        for g in range(GROUPS):
+        def load_columns(g):
             raw = per_group.tile([P, PACK, GROUP_COLS], BF16, name="raw")
+            nc.sync.dma_start(
+                out=raw[:], in_=w_rows[:, :, g * GROUP_COLS : (g + 1) * GROUP_COLS]
+            )
             w_raw.append(raw)
+
         hs = keep.tile([P, HID], BF16)
         nc.sync.dma_start(out=hs[:], in_=hidden_states.rearrange("b s k -> (b s) k"))
-        load_columns(0, 0, GROUP_COLS)
+        load_columns(0)
+        bias_by_head = bq.rearrange("(h d) -> h d", d=HEAD)
+        nc.sync.dma_start(out=rope_bias_rows[0:HEADS, :], in_=bias_by_head[:, NOPE:HEAD])
         nc.sync.dma_start(
-            out=bias_rows[0:HEADS, :], in_=bq.rearrange("(h d) -> h d", d=HEAD)[:, NOPE:HEAD]
-        )
-        nc.sync.dma_start(
-            out=bias_rows[HEADS : HEADS + GROUPS, :].rearrange("g (h d) -> g h d", d=NOPE),
-            in_=bq.rearrange("(g h d) -> g h d", h=GROUP_HEADS, d=HEAD)[:, :, 0:NOPE],
+            out=nope_bias_row[0:1, :].rearrange("p (h d) -> p h d", d=NOPE),
+            in_=bias_by_head[:, 0:NOPE].unsqueeze(0),
         )
         tables = keep.tile([P, 2, ROPE], BF16)
         sin_rows = keep.tile([P, ROPE], BF16)
         nc.sync.dma_start(out=tables[:, 0, :], in_=cos.rearrange("b s d -> (b s) d"))
         nc.sync.dma_start(out=sin_rows[:], in_=sin.rearrange("b s d -> (b s) d"))
         for g in range(1, GROUPS):
-            load_columns(g, 0, GROUP_COLS)
+            load_columns(g)
 
         hs_words = hs[:].bitcast(F32).rearrange("s (p u) -> s u p", u=2)
         hs_grouped = keep.tile([P, P * PACK], BF16, align_bytes=64)
@@ -97,9 +101,8 @@ def tile_gptossmlaattention_pb_s_kernel(tc, hidden_states, cos, sin, Wq, bq, out
         accs_rope = []
         accs_nope = []
         products = {}
-        shifted = {}
+        results = []
         rope_place = {}
-        nope_place = {}
         out_rows = out.rearrange("b h s d -> s (b h) d")
 
         def regroup_piece(copy, g, first_out, first_in, cols):
@@ -138,30 +141,37 @@ def tile_gptossmlaattention_pb_s_kernel(tc, hidden_states, cos, sin, Wq, bq, out
                 in_=w_grouped[g][:, PACK * first : PACK * last],
             )
 
-        def multiply(g, acc, first):
-            nc.tensor.matmul_mx(
-                out=acc,
-                lhsT=w_codes[g][:, first : first + P].bitcast(FP8X4),
-                lhsT_scale=w_scales[g][:, first : first + P],
-                rhs=hs_codes[:].bitcast(FP8X4),
-                rhs_scale=hs_scales[:],
-                start=True,
-                stop=True,
-            )
-
         def project_rope(g):
             new_codes()
             acc_rope = psum_rope.tile([P, GROUP_HEADS, P], F32, name="acc_rope")
             accs_rope.append(acc_rope)
             quantise(g, 0, ROPE_COLS)
             for h in range(GROUP_HEADS):
-                multiply(g, acc_rope[:, h, :], h * ROPE)
+                cols = slice(h * ROPE, (h + 1) * ROPE)
+                nc.tensor.matmul_mx(
+                    out=acc_rope[:, h, :],
+                    lhsT=w_codes[g][:, cols].bitcast(FP8X4),
+                    lhsT_scale=w_scales[g][:, cols],
+                    rhs=hs_codes[:].bitcast(FP8X4),
+                    rhs_scale=hs_scales[:],
+                    start=True,
+                    stop=True,
+                )
 
         def project_nope(g):
-            acc_nope = psum_nope.tile([P, P], F32, name="acc_nope")
-            accs_nope.append(acc_nope)
+            if g % 2 == 0:
+                acc_nope = psum_nope.tile([P, 2, NOPE_COLS], F32, name="acc_nope")
+                accs_nope.append(acc_nope)
             quantise(g, ROPE_COLS, GROUP_COLS)
-            multiply(g, acc_nope[:], ROPE_COLS)
+            nc.tensor.matmul_mx(
+                out=accs_nope[g // 2][:, g % 2, :],
+                lhsT=hs_codes[:].bitcast(FP8X4),
+                lhsT_scale=hs_scales[:],
+                rhs=w_codes[g][:, ROPE_COLS:GROUP_COLS].bitcast(FP8X4),
+                rhs_scale=w_scales[g][:, ROPE_COLS:GROUP_COLS],
+                start=True,
+                stop=True,
+            )
 
         def multiply_by_tables(g, h):
             head = g * GROUP_HEADS + h
@@ -176,22 +186,19 @@ def tile_gptossmlaattention_pb_s_kernel(tc, hidden_states, cos, sin, Wq, bq, out
             )
             products[(g, h)] = by_table
 
-        def add_bias_to_nope(g):
-            plain = per_group.tile([P, P], F32, name="plain")
-            nc.scalar.activation(
-                out=plain[:], in_=accs_nope[g][:], func=ACT.Identity,
-                bias=bias_cols[:, HEADS + g : HEADS + g + 1], scale=1.0,
-            )
-            shifted[g] = plain
+        def new_result():
+            result = per_pair.tile([P, PAIR_HEADS, HEAD], F32, name="result")
+            results.append(result)
 
-        def turn_back_nope(g):
-            nc.tensor.matmul(
-                out=nope_place[g], lhsT=shifted[g][:],
-                rhs=identity.rearrange("p (h d) -> p h d", h=GROUP_HEADS),
-                start=True, stop=True, is_transpose=True,
+        def add_bias_to_nope(pair):
+            nc.vector.tensor_tensor(
+                out=results[pair][:, :, 0:NOPE],
+                in0=accs_nope[pair][:].rearrange("p g (h d) -> p (g h) d", d=NOPE),
+                in1=nope_bias[:, pair * PAIR_HEADS : (pair + 1) * PAIR_HEADS, :],
+                op=ALU.add,
             )
 
-        def turn_back_rope(g, h):
+        def turn_back(g, h):
             nc.tensor.matmul(
                 out=rope_place[(g, h)], lhsT=products[(g, h)][:, 0, :], rhs=identity,
                 start=True, stop=False, is_transpose=True,
@@ -201,24 +208,27 @@ def tile_gptossmlaattention_pb_s_kernel(tc, hidden_states, cos, sin, Wq, bq, out
                 start=False, stop=True, is_transpose=True,
             )
 
-        def new_bank(g):
-            back = psum_turn.tile([P, GROUP_HEADS, HEAD], F32, name="back")
-            for h in range(GROUP_HEADS):
-                rope_place[(g, h)] = back[:, h, NOPE:HEAD]
-            nope_place[g] = back[:, :, 0:NOPE]
+        def new_bank(g, heads):
+            back = psum_turn.tile([P, len(heads), ROPE], F32, name="back")
+            for i, h in enumerate(heads):
+                rope_place[(g, h)] = back[:, i, :]
             return back
 
-        def send(q, g, first_head, heads):
+        def heads_of_pair(g, heads):
+            first = g % 2 * GROUP_HEADS + heads[0]
+            return slice(first, first + len(heads))
+
+        def empty(copy, back, g, heads):
+            copy(out=results[g // 2][:, heads_of_pair(g, heads), NOPE:HEAD], in_=back[:])
+
+        def send(g, heads):
+            first = g * GROUP_HEADS + heads[0]
             nc.sync.dma_start(
-                out=out_rows[:, g * GROUP_HEADS + first_head : g * GROUP_HEADS + first_head + heads, :],
-                in_=q[:, first_head : first_head + heads, :],
+                out=out_rows[:, first : first + len(heads), :],
+                in_=results[g // 2][:, heads_of_pair(g, heads), :],
             )
 
-        def store(back, g):
-            q = per_group.tile([P, GROUP_HEADS, HEAD], F32, name="q")
-            nc.scalar.copy(out=q[:], in_=back[:])
-            send(q, g, 0, GROUP_HEADS)
-
+        both = (0, 1)
         turn_hidden_states()
         nc.scalar.copy(out=tables[:, 1, 0:HALF], in_=sin_rows[:, HALF:ROPE])
         nc.scalar.activation(
@@ -226,17 +236,24 @@ def tile_gptossmlaattention_pb_s_kernel(tc, hidden_states, cos, sin, Wq, bq, out
         )
         for g in range(GROUPS):
             new_grouped()
+        for pair in range(PAIRS):
+            new_result()
         regroup_rope(0, 0)
         regroup_rope(0, 1)
         regroup_nope(0)
+        nope_bias_spread = psum_turn.tile([P, HEADS, NOPE], BF16, name="back")
+        nc.tensor.matmul(
+            out=nope_bias_spread[:].rearrange("p h d -> p (h d)"), lhsT=ones[:], rhs=nope_bias_row,
+            start=True, stop=True,
+        )
         consts_turned = psum_turn.tile([P, 3, P], BF16, name="back")
+        nc.tensor.transpose(consts_turned[:, 2, :], rope_bias_rows, identity_bf[:])
         for t in range(2):
             nc.tensor.transpose(consts_turned[:, t, :], tables[:, t, :], identity_bf[:])
-        nc.tensor.transpose(consts_turned[:, 2, :], bias_rows[:], identity_bf[:])
         tables_turned = keep.tile([P, 2, P], BF16)
         nc.scalar.copy(out=tables_turned[:], in_=consts_turned[:, 0:2, :])
-        bias_cols = keep.tile([P, HEADS + GROUPS], F32)
-        nc.scalar.copy(out=bias_cols[:], in_=consts_turned[:, 2, 0 : HEADS + GROUPS])
+        bias_cols = keep.tile([P, HEADS], F32)
+        nc.scalar.copy(out=bias_cols[:], in_=consts_turned[:, 2, 0:HEADS])
         hs_codes = keep.tile([P, P], U32, align_bytes=64)
         hs_scales = keep.tile([P, P], U8, align_bytes=64)
         nc.vector.quantize_mx(out=hs_codes[:].bitcast(FP8X4), scales=hs_scales[:], in_=hs_grouped[:])
@@ -245,54 +262,44 @@ def tile_gptossmlaattention_pb_s_kernel(tc, hidden_states, cos, sin, Wq, bq, out
         regroup_rope(1, 1)
         project_nope(0)
         regroup_nope(1)
+        nope_bias = keep.tile([P, HEADS, NOPE], BF16)
+        nc.scalar.copy(out=nope_bias[:], in_=nope_bias_spread[:])
         project_rope(1)
         project_nope(1)
-        multiply_by_tables(0, 0)
-        add_bias_to_nope(0)
-        regroup_nope(2)
-        multiply_by_tables(0, 1)
-        multiply_by_tables(1, 0)
-        multiply_by_tables(1, 1)
-        add_bias_to_nope(1)
-        bank_0 = new_bank(0)
-        bank_1 = new_bank(1)
         for g in (0, 1):
-            for h in range(GROUP_HEADS):
-                turn_back_rope(g, h)
-        for g in (0, 1):
-            turn_back_nope(g)
-        regroup_rope(2, 0)
+            for h in both:
+                multiply_by_tables(g, h)
         regroup_rope(2, 1)
+        regroup_nope(2)
+        bank_0 = new_bank(0, both)
+        bank_1 = new_bank(1, both)
+        for g in (0, 1):
+            for h in both:
+                turn_back(g, h)
+        regroup_rope(2, 0)
         regroup_rope(3, 0)
         regroup_rope(3, 1)
         regroup_nope(3)
-        store(bank_0, 0)
-        store(bank_1, 1)
+        add_bias_to_nope(0)
+        empty(nc.scalar.copy, bank_0, 0, both)
+        send(0, both)
+        empty(nc.scalar.copy, bank_1, 1, both)
+        send(1, both)
         project_rope(2)
         project_nope(2)
         project_rope(3)
         project_nope(3)
         for g in (2, 3):
-            multiply_by_tables(g, 0)
-            multiply_by_tables(g, 1)
-            add_bias_to_nope(g)
-        wide_banks = {}
-        narrow_banks = {}
+            for h in both:
+                multiply_by_tables(g, h)
+        add_bias_to_nope(1)
+        banks = {}
         for g in (2, 3):
-            wide_banks[g] = new_bank(g)
-            narrow_banks[g] = psum_turn.tile([P, ROPE], F32, name="back")
-            rope_place[(g, 1)] = narrow_banks[g][:]
-        turn_back_rope(2, 0)
-        turn_back_nope(2)
-        turn_back_rope(2, 1)
-        turn_back_rope(3, 0)
-        turn_back_nope(3)
-        turn_back_rope(3, 1)
+            for h in both:
+                banks[(g, h)] = new_bank(g, (h,))
+                turn_back(g, h)
         for g in (2, 3):
-            q = per_group.tile([P, GROUP_HEADS, HEAD], F32, name="q")
-            q_cols = q[:].rearrange("p h d -> p (h d)")
-            bank_cols = wide_banks[g][:].rearrange("p h d -> p (h d)")
-            nc.scalar.copy(out=q_cols[:, 0 : HEAD + NOPE], in_=bank_cols[:, 0 : HEAD + NOPE])
-            send(q, g, 0, 1)
-            nc.vector.tensor_copy(out=q[:, 1, NOPE:HEAD], in_=narrow_banks[g][:])
-            send(q, g, 1, 1)
+            empty(nc.scalar.copy, banks[(g, 0)], g, (0,))
+            send(g, (0,))
+            empty(nc.vector.tensor_copy, banks[(g, 1)], g, (1,))
+            send(g, (1,))

@@ -28,6 +28,8 @@ PAIRS = 2
 PAIR_HEADS = HEADS // PAIRS
 SCALAR_ROPE = ((2, 1), (3, 1))
 
+LAST = (GROUPS - 1, GROUP_HEADS - 1)
+
 FLOPS = 2 * P * HID * HEADS * HEAD
 
 
@@ -148,12 +150,17 @@ def tile_gptossmlaattention_pb_s_kernel(tc, hidden_states, cos, sin, Wq, bq, out
             quantise(g, 0, ROPE_COLS)
             for h in range(GROUP_HEADS):
                 cols = slice(h * ROPE, (h + 1) * ROPE)
+                columns = (w_codes[g][:, cols].bitcast(FP8X4), w_scales[g][:, cols])
+                positions = (hs_codes[:].bitcast(FP8X4), hs_scales[:])
+                stationary, moving = (
+                    (positions, columns) if (g, h) == LAST else (columns, positions)
+                )
                 nc.tensor.matmul_mx(
                     out=acc_rope[:, h, :],
-                    lhsT=w_codes[g][:, cols].bitcast(FP8X4),
-                    lhsT_scale=w_scales[g][:, cols],
-                    rhs=hs_codes[:].bitcast(FP8X4),
-                    rhs_scale=hs_scales[:],
+                    lhsT=stationary[0],
+                    lhsT_scale=stationary[1],
+                    rhs=moving[0],
+                    rhs_scale=moving[1],
                     start=True,
                     stop=True,
                 )
@@ -241,9 +248,9 @@ def tile_gptossmlaattention_pb_s_kernel(tc, hidden_states, cos, sin, Wq, bq, out
         regroup_rope(0, 0)
         regroup_rope(0, 1)
         regroup_nope(0)
-        nope_bias_spread = psum_turn.tile([P, HEADS, NOPE], BF16, name="back")
+        bias_spread = psum_turn.tile([P, HEADS * NOPE + ROPE], BF16, name="back")
         nc.tensor.matmul(
-            out=nope_bias_spread[:].rearrange("p h d -> p (h d)"), lhsT=ones[:], rhs=nope_bias_row,
+            out=bias_spread[:, 0 : HEADS * NOPE], lhsT=ones[:], rhs=nope_bias_row,
             start=True, stop=True,
         )
         consts_turned = psum_turn.tile([P, 3, P], BF16, name="back")
@@ -252,7 +259,7 @@ def tile_gptossmlaattention_pb_s_kernel(tc, hidden_states, cos, sin, Wq, bq, out
             nc.tensor.transpose(consts_turned[:, t, :], tables[:, t, :], identity_bf[:])
         tables_turned = keep.tile([P, 2, P], BF16)
         nc.scalar.copy(out=tables_turned[:], in_=consts_turned[:, 0:2, :])
-        bias_cols = keep.tile([P, HEADS], F32)
+        bias_cols = keep.tile([P, HEADS], BF16)
         nc.scalar.copy(out=bias_cols[:], in_=consts_turned[:, 2, 0:HEADS])
         hs_codes = keep.tile([P, P], U32, align_bytes=64)
         hs_scales = keep.tile([P, P], U8, align_bytes=64)
@@ -260,16 +267,23 @@ def tile_gptossmlaattention_pb_s_kernel(tc, hidden_states, cos, sin, Wq, bq, out
         project_rope(0)
         regroup_rope(1, 0)
         regroup_rope(1, 1)
+        nc.tensor.transpose(
+            bias_spread[:, HEADS * NOPE :],
+            bias_cols[:, HEADS - 1 : HEADS].to_broadcast([P, P]),
+            identity_bf[:],
+        )
         project_nope(0)
         regroup_nope(1)
-        nope_bias = keep.tile([P, HEADS, NOPE], BF16)
-        nc.scalar.copy(out=nope_bias[:], in_=nope_bias_spread[:])
         project_rope(1)
         project_nope(1)
         for g in (0, 1):
             for h in both:
                 multiply_by_tables(g, h)
         regroup_rope(2, 1)
+        spread_bias = keep.tile([P, HEADS * NOPE + ROPE], BF16)
+        nc.scalar.copy(out=spread_bias[:], in_=bias_spread[:])
+        nope_bias = spread_bias[:, 0 : HEADS * NOPE].rearrange("p (h d) -> p h d", d=NOPE)
+        last_bias = spread_bias[:, HEADS * NOPE :]
         regroup_nope(2)
         bank_0 = new_bank(0, both)
         bank_1 = new_bank(1, both)
@@ -289,17 +303,28 @@ def tile_gptossmlaattention_pb_s_kernel(tc, hidden_states, cos, sin, Wq, bq, out
         project_nope(2)
         project_rope(3)
         project_nope(3)
-        for g in (2, 3):
-            for h in both:
-                multiply_by_tables(g, h)
+        multiply_by_tables(2, 0)
+        multiply_by_tables(2, 1)
+        multiply_by_tables(3, 0)
+        x = keep.tile([P, ROPE], F32)
+        by_cos = keep.tile([P, ROPE], F32)
+        by_sin = keep.tile([P, ROPE], F32)
+        nc.vector.tensor_tensor(out=x[:], in0=accs_rope[3][:, 1, :], in1=last_bias, op=ALU.add)
         add_bias_to_nope(1)
-        banks = {}
-        for g in (2, 3):
-            for h in both:
-                banks[(g, h)] = new_bank(g, (h,))
-                turn_back(g, h)
-        for g in (2, 3):
-            empty(nc.scalar.copy, banks[(g, 0)], g, (0,))
-            send(g, (0,))
-            empty(nc.vector.tensor_copy, banks[(g, 1)], g, (1,))
-            send(g, (1,))
+        nc.vector.scalar_tensor_tensor(
+            out=by_sin[:, 0:HALF], in0=x[:, HALF:ROPE], scalar=-1.0, in1=sin_rows[:, 0:HALF],
+            op0=ALU.mult, op1=ALU.mult,
+        )
+        nc.vector.tensor_tensor(
+            out=by_sin[:, HALF:ROPE], in0=x[:, 0:HALF], in1=sin_rows[:, HALF:ROPE], op=ALU.mult
+        )
+        nc.vector.tensor_tensor(out=by_cos[:], in0=x[:], in1=tables[:, 0, :], op=ALU.mult)
+        nc.vector.tensor_tensor(
+            out=results[1][:, PAIR_HEADS - 1, NOPE:HEAD], in0=by_cos[:], in1=by_sin[:], op=ALU.add
+        )
+        for g, h in ((2, 0), (2, 1), (3, 0)):
+            bank = new_bank(g, (h,))
+            turn_back(g, h)
+            empty(nc.scalar.copy, bank, g, (h,))
+            send(g, (h,))
+        send(3, (1,))

from contextlib import ExitStack

import concourse.mybir as mybir
from concourse.masks import make_identity

BF16 = mybir.dt.bfloat16
F32 = mybir.dt.float32
U32 = mybir.dt.uint32
U8 = mybir.dt.uint8
FP8X4 = mybir.dt.float8_e4m3fn_x4
ALU = mybir.AluOpType
ACT = mybir.ActivationFunctionType

P = 128
PACK = 4
HID = P * PACK
HEADS = 8
NOPE = 64
HALF = 64
ROPE = 2 * HALF
HEAD = NOPE + ROPE
GROUP_HEADS = 2
GROUPS = HEADS // GROUP_HEADS
GROUP_COLS = GROUP_HEADS * HEAD
ROPE_COLS = GROUP_HEADS * ROPE
NOPE_COLS = GROUP_HEADS * NOPE
PAIRS = 2
PAIR_HEADS = HEADS // PAIRS
SCALAR_ROPE = ((2, 1), (3, 1))

LAST = (GROUPS - 1, GROUP_HEADS - 1)

FLOPS = 2 * P * HID * HEADS * HEAD


def tile_gptossmlaattention_pb_s_kernel(tc, hidden_states, cos, sin, Wq, bq, out):
    nc = tc.nc
    with ExitStack() as ctx:
        ctx.enter_context(tc.manual_schedule())
        keep = ctx.enter_context(tc.tile_pool(name="keep", bufs=1))
        per_group = ctx.enter_context(tc.tile_pool(name="per_group", bufs=GROUPS))
        per_pair = ctx.enter_context(tc.tile_pool(name="per_pair", bufs=PAIRS))
        per_head = ctx.enter_context(tc.tile_pool(name="per_head", bufs=HEADS))
        psum_rope = ctx.enter_context(tc.psum_pool(name="psum_rope", bufs=2))
        psum_nope = ctx.enter_context(tc.psum_pool(name="psum_nope", bufs=PAIRS))
        psum_turn = ctx.enter_context(tc.psum_pool(name="psum_turn", bufs=4))

        two_identities = keep.tile([P, 2 * P], F32)
        make_identity(nc, two_identities[:, 0:P])
        identity = two_identities[:, 0:P]
        exchange = two_identities[:, HALF : HALF + P]
        bias_rows = keep.tile([P, ROPE + HEADS * NOPE], BF16)
        nc.vector.memset(bias_rows[:].bitcast(F32), 0.0)
        rope_bias_rows = bias_rows[:, 0:ROPE]
        nope_bias_row = bias_rows[:, ROPE : ROPE + HEADS * NOPE]
        ones = keep.tile([P, P], BF16)
        nc.vector.memset(ones[:], 1.0)
        nc.vector.tensor_copy(out=two_identities[:, P : 2 * P], in_=identity)
        identity_bf = keep.tile([P, P], BF16)
        nc.vector.tensor_copy(out=identity_bf[:], in_=identity)

        w_rows = Wq.rearrange("(p j) n -> p j n", j=PACK)
        w_raw = []

        def load_columns(g):
            raw = per_group.tile([P, PACK, GROUP_COLS], BF16, name="raw")
            nc.sync.dma_start(
                out=raw[:], in_=w_rows[:, :, g * GROUP_COLS : (g + 1) * GROUP_COLS]
            )
            w_raw.append(raw)

        hs = keep.tile([P, HID], BF16)
        nc.sync.dma_start(out=hs[:], in_=hidden_states.rearrange("b s k -> (b s) k"))
        load_columns(0)
        bias_by_head = bq.rearrange("(h d) -> h d", d=HEAD)
        nc.sync.dma_start(out=rope_bias_rows[0:HEADS, :], in_=bias_by_head[:, NOPE:HEAD])
        nc.sync.dma_start(
            out=nope_bias_row[0:1, :].rearrange("p (h d) -> p h d", d=NOPE),
            in_=bias_by_head[:, 0:NOPE].unsqueeze(0),
        )
        tables = keep.tile([P, 2, ROPE], BF16)
        sin_rows = keep.tile([P, ROPE], BF16)
        nc.sync.dma_start(out=tables[:, 0, :], in_=cos.rearrange("b s d -> (b s) d"))
        nc.sync.dma_start(out=sin_rows[:], in_=sin.rearrange("b s d -> (b s) d"))
        for g in range(1, GROUPS):
            load_columns(g)

        hs_words = hs[:].bitcast(F32).rearrange("s (p u) -> s u p", u=2)
        hs_grouped = keep.tile([P, P * PACK], BF16, align_bytes=64)

        def turn_hidden_states():
            hs_turned = psum_turn.tile([P, 2, P], F32, name="back")
            for u in range(2):
                nc.tensor.transpose(hs_turned[:, u, :], hs_words[:, u, :], identity)
            nc.scalar.copy(
                out=hs_grouped[:].bitcast(F32).rearrange("p (s u) -> p s u", u=2),
                in_=hs_turned[:].rearrange("p u s -> p s u"),
            )

        w_grouped = []
        w_codes = []
        w_scales = []
        accs_rope = []
        accs_nope = []
        products = {}
        results = []
        rope_place = {}
        out_rows = out.rearrange("b h s d -> s (b h) d")

        def regroup_piece(copy, g, first_out, first_in, cols):
            copy(
                out=w_grouped[g][:, PACK * first_out : PACK * (first_out + cols)].rearrange(
                    "p (c i j) -> p c j i", i=4, j=PACK
                ),
                in_=w_raw[g][:, :, first_in : first_in + cols].rearrange(
                    "p j (c i) -> p c j i", i=4
                ),
            )

        def new_grouped():
            grouped = per_group.tile([P, GROUP_COLS * PACK], BF16, align_bytes=64, name="grouped")
            w_grouped.append(grouped)

        def regroup_rope(g, h):
            by_scalar = (g, h) in SCALAR_ROPE
            copy = nc.scalar.copy if by_scalar else nc.vector.tensor_copy
            regroup_piece(copy, g, h * ROPE, h * HEAD + NOPE, ROPE)

        def regroup_nope(g):
            for h in range(GROUP_HEADS):
                regroup_piece(nc.scalar.copy, g, ROPE_COLS + h * NOPE, h * HEAD, NOPE)

        def new_codes():
            codes = per_group.tile([P, GROUP_COLS], U32, align_bytes=64, name="codes")
            scales = per_group.tile([P, GROUP_COLS], U8, align_bytes=64, name="scales")
            w_codes.append(codes)
            w_scales.append(scales)

        def quantise(g, first, last):
            nc.vector.quantize_mx(
                out=w_codes[g][:, first:last].bitcast(FP8X4),
                scales=w_scales[g][:, first:last],
                in_=w_grouped[g][:, PACK * first : PACK * last],
            )

        def project_rope(g):
            new_codes()
            acc_rope = psum_rope.tile([P, GROUP_HEADS, P], F32, name="acc_rope")
            accs_rope.append(acc_rope)
            quantise(g, 0, ROPE_COLS)
            for h in range(GROUP_HEADS):
                cols = slice(h * ROPE, (h + 1) * ROPE)
                columns = (w_codes[g][:, cols].bitcast(FP8X4), w_scales[g][:, cols])
                positions = (hs_codes[:].bitcast(FP8X4), hs_scales[:])
                stationary, moving = (
                    (positions, columns) if (g, h) == LAST else (columns, positions)
                )
                nc.tensor.matmul_mx(
                    out=acc_rope[:, h, :],
                    lhsT=stationary[0],
                    lhsT_scale=stationary[1],
                    rhs=moving[0],
                    rhs_scale=moving[1],
                    start=True,
                    stop=True,
                )

        def project_nope(g):
            if g % 2 == 0:
                acc_nope = psum_nope.tile([P, 2, NOPE_COLS], F32, name="acc_nope")
                accs_nope.append(acc_nope)
            quantise(g, ROPE_COLS, GROUP_COLS)
            nc.tensor.matmul_mx(
                out=accs_nope[g // 2][:, g % 2, :],
                lhsT=hs_codes[:].bitcast(FP8X4),
                lhsT_scale=hs_scales[:],
                rhs=w_codes[g][:, ROPE_COLS:GROUP_COLS].bitcast(FP8X4),
                rhs_scale=w_scales[g][:, ROPE_COLS:GROUP_COLS],
                start=True,
                stop=True,
            )

        def multiply_by_tables(g, h):
            head = g * GROUP_HEADS + h
            by_table = per_head.tile([P, 2, P], F32, name="by_table")
            nc.vector.scalar_tensor_tensor(
                out=by_table[:],
                in0=accs_rope[g][:, h, :].unsqueeze(1).to_broadcast([P, 2, P]),
                scalar=bias_cols[:, head : head + 1],
                in1=tables_turned[:],
                op0=ALU.add,
                op1=ALU.mult,
            )
            products[(g, h)] = by_table

        def new_result():
            result = per_pair.tile([P, PAIR_HEADS, HEAD], F32, name="result")
            results.append(result)

        def add_bias_to_nope(pair):
            nc.vector.tensor_tensor(
                out=results[pair][:, :, 0:NOPE],
                in0=accs_nope[pair][:].rearrange("p g (h d) -> p (g h) d", d=NOPE),
                in1=nope_bias[:, pair * PAIR_HEADS : (pair + 1) * PAIR_HEADS, :],
                op=ALU.add,
            )

        def turn_back(g, h):
            nc.tensor.matmul(
                out=rope_place[(g, h)], lhsT=products[(g, h)][:, 0, :], rhs=identity,
                start=True, stop=False, is_transpose=True,
            )
            nc.tensor.matmul(
                out=rope_place[(g, h)], lhsT=products[(g, h)][:, 1, :], rhs=exchange,
                start=False, stop=True, is_transpose=True,
            )

        def new_bank(g, heads):
            back = psum_turn.tile([P, len(heads), ROPE], F32, name="back")
            for i, h in enumerate(heads):
                rope_place[(g, h)] = back[:, i, :]
            return back

        def heads_of_pair(g, heads):
            first = g % 2 * GROUP_HEADS + heads[0]
            return slice(first, first + len(heads))

        def empty(copy, back, g, heads):
            copy(out=results[g // 2][:, heads_of_pair(g, heads), NOPE:HEAD], in_=back[:])

        def send(g, heads):
            first = g * GROUP_HEADS + heads[0]
            nc.sync.dma_start(
                out=out_rows[:, first : first + len(heads), :],
                in_=results[g // 2][:, heads_of_pair(g, heads), :],
            )

        both = (0, 1)
        turn_hidden_states()
        nc.scalar.copy(out=tables[:, 1, 0:HALF], in_=sin_rows[:, HALF:ROPE])
        nc.scalar.activation(
            out=tables[:, 1, HALF:ROPE], in_=sin_rows[:, 0:HALF], func=ACT.Copy, scale=-1.0
        )
        for g in range(GROUPS):
            new_grouped()
        for pair in range(PAIRS):
            new_result()
        regroup_rope(0, 0)
        regroup_rope(0, 1)
        regroup_nope(0)
        bias_spread = psum_turn.tile([P, HEADS * NOPE + ROPE], BF16, name="back")
        nc.tensor.matmul(
            out=bias_spread[:, 0 : HEADS * NOPE], lhsT=ones[:], rhs=nope_bias_row,
            start=True, stop=True,
        )
        consts_turned = psum_turn.tile([P, 3, P], BF16, name="back")
        nc.tensor.transpose(consts_turned[:, 2, :], rope_bias_rows, identity_bf[:])
        for t in range(2):
            nc.tensor.transpose(consts_turned[:, t, :], tables[:, t, :], identity_bf[:])
        tables_turned = keep.tile([P, 2, P], BF16)
        nc.scalar.copy(out=tables_turned[:], in_=consts_turned[:, 0:2, :])
        bias_cols = keep.tile([P, HEADS], BF16)
        nc.scalar.copy(out=bias_cols[:], in_=consts_turned[:, 2, 0:HEADS])
        hs_codes = keep.tile([P, P], U32, align_bytes=64)
        hs_scales = keep.tile([P, P], U8, align_bytes=64)
        nc.vector.quantize_mx(out=hs_codes[:].bitcast(FP8X4), scales=hs_scales[:], in_=hs_grouped[:])
        project_rope(0)
        regroup_rope(1, 0)
        regroup_rope(1, 1)
        nc.tensor.transpose(
            bias_spread[:, HEADS * NOPE :],
            bias_cols[:, HEADS - 1 : HEADS].to_broadcast([P, P]),
            identity_bf[:],
        )
        project_nope(0)
        regroup_nope(1)
        project_rope(1)
        project_nope(1)
        for g in (0, 1):
            for h in both:
                multiply_by_tables(g, h)
        regroup_rope(2, 1)
        spread_bias = keep.tile([P, HEADS * NOPE + ROPE], BF16)
        nc.scalar.copy(out=spread_bias[:], in_=bias_spread[:])
        nope_bias = spread_bias[:, 0 : HEADS * NOPE].rearrange("p (h d) -> p h d", d=NOPE)
        last_bias = spread_bias[:, HEADS * NOPE :]
        regroup_nope(2)
        bank_0 = new_bank(0, both)
        bank_1 = new_bank(1, both)
        for g in (0, 1):
            for h in both:
                turn_back(g, h)
        regroup_rope(2, 0)
        regroup_rope(3, 0)
        regroup_rope(3, 1)
        regroup_nope(3)
        add_bias_to_nope(0)
        empty(nc.scalar.copy, bank_0, 0, both)
        send(0, both)
        empty(nc.scalar.copy, bank_1, 1, both)
        send(1, both)
        project_rope(2)
        project_nope(2)
        project_rope(3)
        project_nope(3)
        multiply_by_tables(2, 0)
        multiply_by_tables(2, 1)
        multiply_by_tables(3, 0)
        x = keep.tile([P, ROPE], F32)
        by_cos = keep.tile([P, ROPE], F32)
        by_sin = keep.tile([P, ROPE], F32)
        nc.vector.tensor_tensor(out=x[:], in0=accs_rope[3][:, 1, :], in1=last_bias, op=ALU.add)
        add_bias_to_nope(1)
        nc.vector.scalar_tensor_tensor(
            out=by_sin[:, 0:HALF], in0=x[:, HALF:ROPE], scalar=-1.0, in1=sin_rows[:, 0:HALF],
            op0=ALU.mult, op1=ALU.mult,
        )
        nc.vector.tensor_tensor(
            out=by_sin[:, HALF:ROPE], in0=x[:, 0:HALF], in1=sin_rows[:, HALF:ROPE], op=ALU.mult
        )
        nc.vector.tensor_tensor(out=by_cos[:], in0=x[:], in1=tables[:, 0, :], op=ALU.mult)
        nc.vector.tensor_tensor(
            out=results[1][:, PAIR_HEADS - 1, NOPE:HEAD], in0=by_cos[:], in1=by_sin[:], op=ALU.add
        )
        for g, h in ((2, 0), (2, 1), (3, 0)):
            bank = new_bank(g, (h,))
            turn_back(g, h)
            empty(nc.scalar.copy, bank, g, (h,))
            send(g, (h,))
        send(3, (1,))
